import numpy as np
import ml_dtypes


def mxq(x, axis, fmt="e4m3"):
    dtype, down = {"e4m3": (ml_dtypes.float8_e4m3fn, 7), "e5m2": (ml_dtypes.float8_e5m2, 14)}[fmt]
    v = np.moveaxis(np.asarray(x, np.float32).astype(ml_dtypes.bfloat16).astype(np.float64), axis, -1)
    blocks = v.reshape(v.shape[:-1] + (-1, 32))
    amax = np.abs(blocks).max(-1, keepdims=True)
    byte = np.maximum(np.where(amax > 0, np.frexp(amax)[1] - 1 + 127, 0) - down, 1)
    scale = np.exp2(byte - 127.0)
    codes = (blocks / scale).astype(np.float32).astype(dtype).astype(np.float64)
    return np.moveaxis((codes * scale).reshape(v.shape), -1, axis)


WIDE = False


def mx_kscale(k):
    if not WIDE:
        return np.ones(k)
    levels = np.array([10, -10, 5, -5, 0])
    if k % 512:
        return np.exp2(np.random.permutation(np.resize(levels, k // 32))).repeat(32)
    a = np.empty((k // 512, 16))
    for p in range(k // 512):
        a[p, :8] = np.random.permutation(np.resize(levels, 8))
        for g in range(8):
            far = levels[np.abs(levels - a[p, g]) >= 10]
            a[p, g + 8] = far[np.random.randint(len(far))]
    return np.exp2(a.ravel()).repeat(32)


BF16 = ml_dtypes.bfloat16


def bf(x):
    return np.asarray(x, np.float32).astype(BF16)


def f64(x):
    return np.asarray(x).astype(np.float64)


B, S, HID, NH, NOPE, ROPE, VD, KV_RANK, SW, QB = 1, 8192, 512, 2, 64, 128, 128, 512, 384, 128


def rotate_half(x):
    h = x.shape[-1] // 2
    return np.concatenate([-x[..., h:], x[..., :h]], axis=-1)


def rope_tables():
    pos = np.arange(S, dtype=np.float64)
    inv = 1.0 / (10000.0 ** (np.arange(0, ROPE, 2, dtype=np.float64) / ROPE))
    ang = pos[:, None] * inv[None, :]
    ang = np.concatenate([ang, ang], axis=-1)
    return bf(np.broadcast_to(np.cos(ang)[None], (B, S, ROPE))), bf(np.broadcast_to(np.sin(ang)[None], (B, S, ROPE)))


def draw0():
    s, t = mx_kscale(HID), mx_kscale(KV_RANK)
    col = np.concatenate([t, np.ones(ROPE)])
    cos, sin = rope_tables()
    return {"hidden_states": bf(np.random.standard_normal((B, S, HID)) * s), "cos": cos, "sin": sin,
            "Wkva": bf(np.random.standard_normal((HID, KV_RANK + ROPE)) / np.sqrt(HID) / s[:, None] * col),
            "bkva": bf(np.random.standard_normal(KV_RANK + ROPE) * 0.1 * col),
            "Wkvb": bf(np.random.standard_normal((KV_RANK, NH * (NOPE + VD))) / np.sqrt(KV_RANK) / t[:, None])}


def core(hidden_states, cos, sin, Wkva, bkva, Wkvb):
    ckv = (mxq(f64(hidden_states), 2, "e4m3") @ mxq(f64(Wkva), 0, "e4m3")) + f64(bkva)
    kv_lat, k_rope = ckv[..., :KV_RANK], ckv[..., KV_RANK:]
    kv = (mxq(kv_lat, 2, "e4m3") @ mxq(f64(Wkvb), 0, "e4m3")).reshape(B, S, NH, NOPE + VD).transpose(0, 2, 1, 3)
    k_nope, v = kv[..., :NOPE], kv[..., NOPE:]
    k_rope = k_rope.reshape(B, 1, S, ROPE)
    c, si = f64(cos)[:, None], f64(sin)[:, None]
    k_rope = k_rope * c + rotate_half(k_rope) * si
    k_rope = np.broadcast_to(k_rope, (B, NH, S, ROPE))
    kk = np.concatenate([k_nope, k_rope], axis=-1)
    return kk, np.ascontiguousarray(v)


def e4m3fn_bytes(y):
    return np.clip(np.asarray(y, np.float64), -448.0, 448.0).astype(np.float32).astype(ml_dtypes.float8_e4m3fn).view(np.uint8)


def e4m3fn_values(b):
    return np.asarray(b, np.uint8).view(ml_dtypes.float8_e4m3fn).astype(np.float64)


def setup_inputs():
    d = draw0()
    x0 = np.asarray(d['hidden_states']).astype(np.float64)
    s = (np.max(np.abs(x0), axis=(0, 1), keepdims=True) / 448.0).astype(np.float32)
    out = {}
    for k, v in d.items():
        if k == 'hidden_states':
            out['hidden_states_bytes'] = e4m3fn_bytes(x0 / s.astype(np.float64))
            out['hidden_states_scale'] = s
        else:
            out[k] = v
    return out


def reference(hidden_states_bytes, hidden_states_scale, cos, sin, Wkva, bkva, Wkvb):
    return core(e4m3fn_values(hidden_states_bytes) * hidden_states_scale.astype(np.float64), cos, sin, Wkva, bkva, Wkvb)

@@ -1,0 +1,361 @@
+from contextlib import ExitStack
+
+import concourse.mybir as mybir
+from concourse.masks import make_identity
+
+F32 = mybir.dt.float32
+BF16 = mybir.dt.bfloat16
+U32 = mybir.dt.uint32
+U8 = mybir.dt.uint8
+FP8 = mybir.dt.float8_e4m3fn
+FP8X4 = mybir.dt.float8_e4m3fn_x4
+MULT = mybir.AluOpType.mult
+ADD = mybir.AluOpType.add
+SUB = mybir.AluOpType.subtract
+IDENT = mybir.ActivationFunctionType.Identity
+
+P = 128
+S, K, R = 8192, 512, 512
+ROPE, NOPE, VD, NH = 128, 64, 128, 2
+TPP = S // P
+TB = 4
+NB = TPP // TB
+CHUNK = 8
+
+FLOPS = 2 * S * K * (R + ROPE) + 2 * S * R * NH * (NOPE + VD)
+
+
+def tile_gptossmlaattention_pa_t_kernel(tc, x_bytes, x_scale, cos, sin, wkva, bkva, wkvb, kk_out, v_out):
+    nc = tc.nc
+    with ExitStack() as ctx:
+        ctx.enter_context(tc.manual_schedule())
+        keep = ctx.enter_context(tc.tile_pool(name="keep", bufs=1))
+        xin = ctx.enter_context(tc.tile_pool(name="xin", bufs=1))
+        p2 = ctx.enter_context(tc.tile_pool(name="p2", bufs=2))
+        p3 = ctx.enter_context(tc.tile_pool(name="p3", bufs=3))
+        outp = ctx.enter_context(tc.tile_pool(name="outp", bufs=4))
+        ps_x = ctx.enter_context(tc.psum_pool(name="ps_x", bufs=2))
+        ps_l = ctx.enter_context(tc.psum_pool(name="ps_l", bufs=3))
+        ps_r = ctx.enter_context(tc.psum_pool(name="ps_r", bufs=1))
+        ps_kv = ctx.enter_context(tc.psum_pool(name="ps_kv", bufs=2))
+
+        x_rows = x_bytes.rearrange("o (p s) k -> p (o s k)", p=P)
+        cos_rows = cos.rearrange("o (p s) c -> p (o s c)", p=P)
+        sin_rows = sin.rearrange("o (p s) c -> p (o s c)", p=P)
+        kk_rows = kk_out.rearrange("o h (p s) c -> p (o h) (s c)", p=P)
+        v_rows = v_out.rearrange("o h (p s) c -> p (o h) (s c)", p=P)
+
+        x_sb = []
+        c_sb = []
+        s_sb = []
+        for g in range(TPP // CHUNK):
+            xt = xin.tile([P, CHUNK * K], U8, name="x%d" % g)
+            ct = xin.tile([P, CHUNK * ROPE], BF16, name="c%d" % g)
+            st = xin.tile([P, CHUNK * ROPE], BF16, name="s%d" % g)
+            x_sb.append(xt)
+            c_sb.append(ct)
+            s_sb.append(st)
+
+        def load_x(g, lo, hi):
+            nc.sync.dma_start(out=x_sb[g][:, lo * K : hi * K], in_=x_rows[:, (g * CHUNK + lo) * K : (g * CHUNK + hi) * K])
+
+        def load_cs(g):
+            cols = slice(g * CHUNK * ROPE, (g + 1) * CHUNK * ROPE)
+            nc.sync.dma_start(out=c_sb[g][:], in_=cos_rows[:, cols])
+            nc.sync.dma_start(out=s_sb[g][:], in_=sin_rows[:, cols])
+
+        wa_raw = keep.tile([P, 4, R + ROPE], BF16, name="wa_raw")
+        wb_raw = keep.tile([P, 4, NH * (NOPE + VD)], BF16, name="wb_raw")
+        scale = keep.tile([P, 4], F32, name="scale")
+        bias_l = keep.tile([P, 4], BF16, name="bias_l")
+        bias_r = keep.tile([P, ROPE], BF16, name="bias_r")
+        load_x(0, 0, 4)
+        nc.sync.dma_start(out=wa_raw[:], in_=wkva.rearrange("(p j) w -> p j w", j=4))
+        nc.sync.dma_start(out=scale[:], in_=x_scale.rearrange("a b (p t) -> p (a b t)", t=4))
+        nc.sync.dma_start(out=bias_l[:], in_=bkva[0:R].rearrange("(p t) -> p t", t=4))
+        nc.sync.dma_start(out=bias_r[:], in_=bkva[R : R + ROPE].partition_broadcast(P))
+        load_x(0, 4, 8)
+        nc.sync.dma_start(out=wb_raw[:], in_=wkvb.rearrange("(p j) w -> p j w", j=4))
+        load_cs(0)
+        for g in range(1, TPP // CHUNK):
+            load_x(g, 0, CHUNK)
+            load_cs(g)
+
+        ident = keep.tile([P, P], F32, name="ident")
+        make_identity(nc, ident[:])
+        warm = keep.tile([P, 1], F32, name="warm")
+        nc.vector.memset(warm[:], 0.0)
+        nc.scalar.activation(out=warm[:], in_=warm[:], func=IDENT)
+
+        wa_g = keep.tile([P, R * 4], BF16, align_bytes=64, name="wa_g")
+        wr_g = keep.tile([P, ROPE * 4], BF16, align_bytes=64, name="wr_g")
+        wn_g = keep.tile([P, NH * NOPE * 4], BF16, align_bytes=64, name="wn_g")
+        wv_g = keep.tile([P, NH * VD * 4], BF16, align_bytes=64, name="wv_g")
+        wa_c = keep.tile([P, R], U32, align_bytes=64, name="wa_c")
+        wa_s = keep.tile([P, R], U8, align_bytes=64, name="wa_s")
+        wr_c = keep.tile([P, ROPE], U32, align_bytes=64, name="wr_c")
+        wr_s = keep.tile([P, ROPE], U8, align_bytes=64, name="wr_s")
+        wn_c = keep.tile([P, NH * NOPE], U32, align_bytes=64, name="wn_c")
+        wn_s = keep.tile([P, NH * NOPE], U8, align_bytes=64, name="wn_s")
+        wv_c = keep.tile([P, NH * VD], U32, align_bytes=64, name="wv_c")
+        wv_s = keep.tile([P, NH * VD], U8, align_bytes=64, name="wv_s")
+
+        def quant(codes, scales, src):
+            nc.vector.quantize_mx(out=codes.bitcast(FP8X4), scales=scales, in_=src)
+
+        def prep_wa():
+            src = wa_raw[:, :, 0:R].rearrange("p j (m t) -> p t m j", t=4)
+            dst = wa_g[:].rearrange("p (t m j) -> p t m j", t=4, j=4)
+            for t in range(4):
+                nc.vector.tensor_copy(out=dst[:, t], in_=src[:, t])
+            nc.vector.tensor_copy(out=wr_g[:].rearrange("p (c j) -> p c j", j=4), in_=wa_raw[:, :, R:].rearrange("p j c -> p c j"))
+            quant(wa_c[:], wa_s[:], wa_g[:])
+            quant(wr_c[:], wr_s[:], wr_g[:])
+
+        def prep_wb():
+            src = wb_raw[:].rearrange("p j (h w) -> p h w j", h=NH)
+            for h in range(NH):
+                nc.vector.tensor_copy(out=wn_g[:].rearrange("p (h c j) -> p h c j", h=NH, j=4)[:, h], in_=src[:, h, 0:NOPE])
+                nc.vector.tensor_copy(out=wv_g[:].rearrange("p (h c j) -> p h c j", h=NH, j=4)[:, h], in_=src[:, h, NOPE:])
+            quant(wn_c[:], wn_s[:], wn_g[:])
+            quant(wv_c[:], wv_s[:], wv_g[:])
+
+        xw, xps, xg, xc, xs = {}, {}, {}, {}, {}
+        lps, lpl, lg, lc, ls = {}, {}, {}, {}, {}
+        rps, krb, kvps, kk, vt = {}, {}, {}, {}, {}
+
+        def ok(b):
+            return 0 <= b < NB
+
+        def cast(b, h):
+            if not ok(b):
+                return
+            if h == 0:
+                t_xw = p3.tile([P, TB, K], BF16, align_bytes=64, name="t_xw")
+                xw[b] = t_xw
+            g, o = divmod(b * TB + 2 * h, CHUNK)
+            src = x_sb[g][:, o * K : (o + 2) * K].bitcast(FP8)
+            dst = xw[b][:, 2 * h : 2 * h + 2, :].rearrange("p j k -> p (j k)")
+            if b == 0:
+                nc.vector.tensor_copy(out=dst, in_=src)
+            else:
+                nc.scalar.copy(out=dst, in_=src)
+
+        def trans(b, h):
+            if not ok(b):
+                return
+            t_xps = ps_x.tile([P, 2, 2 * P], F32, name="t_xps")
+            xps[b, h] = t_xps
+            for jj in range(2):
+                words = xw[b][:, 2 * h + jj, :].bitcast(F32)
+                for u in range(2):
+                    nc.tensor.transpose(t_xps[:, u, jj * P : (jj + 1) * P], words[:, u : K // 2 : 2], ident[:])
+
+        def mulx(b, h):
+            if not ok(b):
+                return
+            if h == 0:
+                t_xg = p2.tile([P, TB * P * 4], BF16, align_bytes=64, name="t_xg")
+                xg[b] = t_xg
+            nc.vector.tensor_tensor(
+                out=xg[b][:, h * 1024 : (h + 1) * 1024].rearrange("p (c u e) -> p c u e", u=2, e=2),
+                in0=xps[b, h][:].bitcast(BF16).rearrange("p u (c e) -> p c u e", e=2),
+                in1=scale[:].unsqueeze(1).to_broadcast([P, 2 * P, 4]).rearrange("p c (u e) -> p c u e", e=2),
+                op=MULT,
+            )
+
+        def quant_x(b):
+            if not ok(b):
+                return
+            t_xc = p3.tile([P, TB * P], U32, align_bytes=64, name="t_xc")
+            t_xs = p3.tile([P, TB * P], U8, align_bytes=64, name="t_xs")
+            xc[b], xs[b] = t_xc, t_xs
+            quant(t_xc[:], t_xs[:], xg[b][:])
+
+        def lat_pair(b, t0):
+            if not ok(b):
+                return
+            t_lps = ps_l.tile([P, 2, 2 * P], F32, name="t_lps")
+            lps[b, "s", t0] = t_lps
+            for t in (t0, t0 + 1):
+                w = slice(t * P, (t + 1) * P)
+                nc.tensor.matmul_mx(
+                    out=t_lps[:, t - t0, :], lhsT=wa_c[:, w].bitcast(FP8X4), lhsT_scale=wa_s[:, w],
+                    rhs=xc[b][:, 0 : 2 * P].bitcast(FP8X4), rhs_scale=xs[b][:, 0 : 2 * P], start=True, stop=True)
+
+        def lat_tile(b, j):
+            if not ok(b):
+                return
+            t_lps = ps_l.tile([P, 4, P], F32, name="t_lps")
+            lps[b, "v", j] = t_lps
+            n = slice(j * P, (j + 1) * P)
+            for t in range(4):
+                w = slice(t * P, (t + 1) * P)
+                nc.tensor.matmul_mx(
+                    out=t_lps[:, t, :], lhsT=wa_c[:, w].bitcast(FP8X4), lhsT_scale=wa_s[:, w],
+                    rhs=xc[b][:, n].bitcast(FP8X4), rhs_scale=xs[b][:, n], start=True, stop=True)
+
+        def rope_mm(b):
+            if not ok(b):
+                return
+            t_rps = ps_r.tile([P, TB, ROPE], F32, name="t_rps")
+            rps[b] = t_rps
+            for j in range(TB):
+                n = slice(j * P, (j + 1) * P)
+                nc.tensor.matmul_mx(
+                    out=t_rps[:, j, :], lhsT=xc[b][:, n].bitcast(FP8X4), lhsT_scale=xs[b][:, n],
+                    rhs=wr_c[:].bitcast(FP8X4), rhs_scale=wr_s[:], start=True, stop=True)
+
+        def evac_s(b, t0):
+            if not ok(b):
+                return
+            if t0 == 0:
+                t_lpl = p2.tile([P, 4, 2 * P], BF16, align_bytes=64, name="t_lpl")
+                lpl[b] = t_lpl
+            for t in (t0, t0 + 1):
+                nc.scalar.activation(out=lpl[b][:, t, :], in_=lps[b, "s", t0][:, t - t0, :], func=IDENT, bias=bias_l[:, t : t + 1])
+
+        def new_lg(b):
+            if not ok(b):
+                return
+            t_lg = p2.tile([P, TB * P * 4], BF16, align_bytes=64, name="t_lg")
+            lg[b] = t_lg
+
+        def inter(b):
+            if not ok(b):
+                return
+            nc.vector.tensor_copy(out=lg[b][:, 0:1024].rearrange("p (n t) -> p n t", t=4), in_=lpl[b][:].rearrange("p t n -> p n t"))
+
+        def evac_v(b, j):
+            if not ok(b):
+                return
+            nc.vector.tensor_tensor(
+                out=lg[b][:, j * 512 : (j + 1) * 512].rearrange("p (n t) -> p n t", t=4),
+                in0=lps[b, "v", j][:].rearrange("p t n -> p n t"),
+                in1=bias_l[:].unsqueeze(1).to_broadcast([P, P, 4]), op=ADD)
+
+        def bias_rope(b):
+            if not ok(b):
+                return
+            t_krb = p2.tile([P, TB, ROPE], F32, name="t_krb")
+            krb[b] = t_krb
+            nc.vector.tensor_tensor(out=t_krb[:], in0=rps[b][:], in1=bias_r[:].unsqueeze(1).to_broadcast([P, TB, ROPE]), op=ADD)
+
+        def quant_l(b):
+            if not ok(b):
+                return
+            t_lc = p2.tile([P, TB * P], U32, align_bytes=64, name="t_lc")
+            t_ls = p2.tile([P, TB * P], U8, align_bytes=64, name="t_ls")
+            lc[b], ls[b] = t_lc, t_ls
+            quant(t_lc[:], t_ls[:], lg[b][:])
+
+        def kv_mm(b, part):
+            if not ok(b):
+                return
+            t_kv = ps_kv.tile([P, 512], F32, name="t_kv")
+            kvps[b, part] = t_kv
+            tiles = range(TB) if part == 0 else (2 * part - 2, 2 * part - 1)
+            wc, ws, width = (wn_c, wn_s, 128) if part == 0 else (wv_c, wv_s, 256)
+            for i, j in enumerate(tiles):
+                n = slice(j * P, (j + 1) * P)
+                nc.tensor.matmul_mx(
+                    out=t_kv[:, i * width : (i + 1) * width], lhsT=lc[b][:, n].bitcast(FP8X4), lhsT_scale=ls[b][:, n],
+                    rhs=wc[:].bitcast(FP8X4), rhs_scale=ws[:], start=True, stop=True)
+
+        def new_out(b):
+            if not ok(b):
+                return
+            t_kk = outp.tile([P, NH, TB, NOPE + ROPE], F32, name="t_kk")
+            t_v = outp.tile([P, NH, TB, VD], F32, name="t_v")
+            kk[b], vt[b] = t_kk, t_v
+
+        def kv_evac(b, part):
+            if not ok(b):
+                return
+            if part == 0:
+                nc.scalar.copy(out=kk[b][:, :, :, 0:NOPE].rearrange("p h j c -> p j h c"),
+                               in_=kvps[b, 0][:].rearrange("p (j h c) -> p j h c", j=TB, h=NH))
+            else:
+                nc.scalar.copy(out=vt[b][:, :, 2 * part - 2 : 2 * part, :].rearrange("p h j c -> p j h c"),
+                               in_=kvps[b, part][:].rearrange("p (j h c) -> p j h c", j=2, h=NH))
+
+        def rope(b):
+            if not ok(b):
+                return
+            g, o = divmod(b * TB, CHUNK)
+            c = c_sb[g][:].rearrange("p (s c) -> p s c", c=ROPE)[:, o : o + TB, :]
+            s = s_sb[g][:].rearrange("p (s c) -> p s c", c=ROPE)[:, o : o + TB, :]
+            m1 = p2.tile([P, TB, ROPE], F32, name="m1")
+            m2 = p2.tile([P, TB, ROPE], F32, name="m2")
+            k = krb[b]
+            hf = ROPE // 2
+            nc.gpsimd.tensor_tensor(out=m1[:], in0=k[:], in1=c, op=MULT)
+            nc.gpsimd.tensor_tensor(out=m2[:, :, 0:hf], in0=k[:, :, hf:], in1=s[:, :, 0:hf], op=MULT)
+            nc.gpsimd.tensor_tensor(out=m2[:, :, hf:], in0=k[:, :, 0:hf], in1=s[:, :, hf:], op=MULT)
+            nc.gpsimd.tensor_tensor(out=kk[b][:, 0, :, NOPE : NOPE + hf], in0=m1[:, :, 0:hf], in1=m2[:, :, 0:hf], op=SUB)
+            nc.gpsimd.tensor_tensor(out=kk[b][:, 0, :, NOPE + hf :], in0=m1[:, :, hf:], in1=m2[:, :, hf:], op=ADD)
+
+        def dup(b):
+            if not ok(b):
+                return
+            nc.scalar.copy(out=kk[b][:, 1, :, NOPE:], in_=kk[b][:, 0, :, NOPE:])
+
+        def store_v(b):
+            if not ok(b):
+                return
+            w = TB * VD
+            nc.sync.dma_start(out=v_rows[:, :, b * w : (b + 1) * w], in_=vt[b][:].rearrange("p h j c -> p h (j c)"))
+
+        def store_kk(b):
+            if not ok(b):
+                return
+            w = TB * (NOPE + ROPE)
+            nc.sync.dma_start(out=kk_rows[:, :, b * w : (b + 1) * w], in_=kk[b][:].rearrange("p h j c -> p h (j c)"))
+
+        cast(0, 0)
+        cast(0, 1)
+        trans(0, 0)
+        trans(0, 1)
+        prep_wa()
+        cast(1, 0)
+        cast(1, 1)
+        mulx(0, 0)
+        mulx(0, 1)
+        trans(1, 0)
+        trans(1, 1)
+        cast(2, 0)
+        cast(2, 1)
+        quant_x(0)
+        prep_wb()
+        for i in range(NB + 2):
+            new_lg(i)
+            new_out(i - 1)
+            lat_pair(i, 0)
+            lat_pair(i, 2)
+            evac_s(i, 0)
+            mulx(i + 1, 0)
+            lat_tile(i, 2)
+            rope_mm(i)
+            evac_s(i, 2)
+            evac_v(i, 2)
+            mulx(i + 1, 1)
+            kv_mm(i - 1, 0)
+            kv_evac(i - 1, 0)
+            lat_tile(i, 3)
+            kv_mm(i - 1, 1)
+            kv_evac(i - 1, 1)
+            inter(i)
+            trans(i + 2, 0)
+            trans(i + 2, 1)
+            quant_x(i + 1)
+            evac_v(i, 3)
+            rope(i - 1)
+            kv_mm(i - 1, 2)
+            kv_evac(i - 1, 2)
+            store_v(i - 1)
+            cast(i + 3, 0)
+            cast(i + 3, 1)
+            bias_rope(i)
+            quant_l(i)
+            dup(i - 1)
+            store_kk(i - 1)

@@ -43,6 +43,7 @@ def tile_gptossmlaattention_pa_t_kernel(tc, x_bytes, x_scale, cos, sin, wkva, bk
         cos_rows = cos.rearrange("o (p s) c -> p (o s c)", p=P)
         sin_rows = sin.rearrange("o (p s) c -> p (o s c)", p=P)
         kk_rows = kk_out.rearrange("o h (p s) c -> p (o h) (s c)", p=P)
+        kk1_rows = kk_out[:, 1].rearrange("o (p s) c -> p (o s) c", p=P)
         v_rows = v_out.rearrange("o h (p s) c -> p (o h) (s c)", p=P)
 
         x_sb = []
@@ -68,12 +69,12 @@ def tile_gptossmlaattention_pa_t_kernel(tc, x_bytes, x_scale, cos, sin, wkva, bk
         wb_raw = keep.tile([P, 4, NH * (NOPE + VD)], BF16, name="wb_raw")
         scale = keep.tile([P, 4], F32, name="scale")
         bias_l = keep.tile([P, 4], BF16, name="bias_l")
-        bias_r = keep.tile([P, ROPE], BF16, name="bias_r")
+        bias_r = keep.tile([P, 1], BF16, name="bias_r")
         load_x(0, 0, 4)
         nc.sync.dma_start(out=wa_raw[:], in_=wkva.rearrange("(p j) w -> p j w", j=4))
         nc.sync.dma_start(out=scale[:], in_=x_scale.rearrange("a b (p t) -> p (a b t)", t=4))
         nc.sync.dma_start(out=bias_l[:], in_=bkva[0:R].rearrange("(p t) -> p t", t=4))
-        nc.sync.dma_start(out=bias_r[:], in_=bkva[R : R + ROPE].partition_broadcast(P))
+        nc.sync.dma_start(out=bias_r[:], in_=bkva[R : R + ROPE].rearrange("(p o) -> p o", o=1))
         load_x(0, 4, 8)
         nc.sync.dma_start(out=wb_raw[:], in_=wkvb.rearrange("(p j) w -> p j w", j=4))
         load_cs(0)
@@ -122,7 +123,7 @@ def tile_gptossmlaattention_pa_t_kernel(tc, x_bytes, x_scale, cos, sin, wkva, bk
 
         xw, xps, xg, xc, xs = {}, {}, {}, {}, {}
         lps, lpl, lg, lc, ls = {}, {}, {}, {}, {}
-        rps, krb, kvps, kk, vt = {}, {}, {}, {}, {}
+        rps, kt, krb, kvps, kk, vt = {}, {}, {}, {}, {}, {}
 
         def ok(b):
             return 0 <= b < NB
@@ -198,13 +199,27 @@ def tile_gptossmlaattention_pa_t_kernel(tc, x_bytes, x_scale, cos, sin, wkva, bk
         def rope_mm(b):
             if not ok(b):
                 return
-            t_rps = ps_r.tile([P, TB, ROPE], F32, name="t_rps")
+            t_rps = ps_r.tile([P, TB * P], F32, name="t_rps")
+            rps[b] = t_rps
+            nc.tensor.matmul_mx(
+                out=t_rps[:], lhsT=wr_c[:].bitcast(FP8X4), lhsT_scale=wr_s[:],
+                rhs=xc[b][:].bitcast(FP8X4), rhs_scale=xs[b][:], start=True, stop=True)
+
+        def rope_evac(b):
+            if not ok(b):
+                return
+            t_kt = p2.tile([P, TB * P], F32, name="t_kt")
+            kt[b] = t_kt
+            nc.scalar.activation(out=t_kt[:], in_=rps[b][:], func=IDENT, bias=bias_r[:])
+
+        def rope_trans(b):
+            if not ok(b):
+                return
+            t_rps = ps_r.tile([P, TB * P], F32, name="t_rps")
             rps[b] = t_rps
             for j in range(TB):
                 n = slice(j * P, (j + 1) * P)
-                nc.tensor.matmul_mx(
-                    out=t_rps[:, j, :], lhsT=xc[b][:, n].bitcast(FP8X4), lhsT_scale=xs[b][:, n],
-                    rhs=wr_c[:].bitcast(FP8X4), rhs_scale=wr_s[:], start=True, stop=True)
+                nc.tensor.transpose(t_rps[:, n], kt[b][:, n], ident[:])
 
         def evac_s(b, t0):
             if not ok(b):
@@ -239,7 +254,7 @@ def tile_gptossmlaattention_pa_t_kernel(tc, x_bytes, x_scale, cos, sin, wkva, bk
                 return
             t_krb = p2.tile([P, TB, ROPE], F32, name="t_krb")
             krb[b] = t_krb
-            nc.vector.tensor_tensor(out=t_krb[:], in0=rps[b][:], in1=bias_r[:].unsqueeze(1).to_broadcast([P, TB, ROPE]), op=ADD)
+            nc.scalar.copy(out=t_krb[:].rearrange("p j c -> p (j c)"), in_=rps[b][:])
 
         def quant_l(b):
             if not ok(b):
@@ -295,11 +310,6 @@ def tile_gptossmlaattention_pa_t_kernel(tc, x_bytes, x_scale, cos, sin, wkva, bk
             nc.gpsimd.tensor_tensor(out=kk[b][:, 0, :, NOPE : NOPE + hf], in0=m1[:, :, 0:hf], in1=m2[:, :, 0:hf], op=SUB)
             nc.gpsimd.tensor_tensor(out=kk[b][:, 0, :, NOPE + hf :], in0=m1[:, :, hf:], in1=m2[:, :, hf:], op=ADD)
 
-        def dup(b):
-            if not ok(b):
-                return
-            nc.scalar.copy(out=kk[b][:, 1, :, NOPE:], in_=kk[b][:, 0, :, NOPE:])
-
         def store_v(b):
             if not ok(b):
                 return
@@ -310,7 +320,13 @@ def tile_gptossmlaattention_pa_t_kernel(tc, x_bytes, x_scale, cos, sin, wkva, bk
             if not ok(b):
                 return
             w = TB * (NOPE + ROPE)
-            nc.sync.dma_start(out=kk_rows[:, :, b * w : (b + 1) * w], in_=kk[b][:].rearrange("p h j c -> p h (j c)"))
+            nc.sync.dma_start(out=kk_rows[:, 0, b * w : (b + 1) * w], in_=kk[b][:, 0].rearrange("p j c -> p (j c)"))
+            nc.sync.dma_start(out=kk1_rows[:, b * TB : (b + 1) * TB, NOPE:], in_=kk[b][:, 0, :, NOPE:])
+
+        def store_k1(b):
+            if not ok(b):
+                return
+            nc.sync.dma_start(out=kk1_rows[:, b * TB : (b + 1) * TB, 0:NOPE], in_=kk[b][:, 1, :, 0:NOPE])
 
         cast(0, 0)
         cast(0, 1)
@@ -334,9 +350,10 @@ def tile_gptossmlaattention_pa_t_kernel(tc, x_bytes, x_scale, cos, sin, wkva, bk
             lat_pair(i, 2)
             evac_s(i, 0)
             mulx(i + 1, 0)
-            lat_tile(i, 2)
             rope_mm(i)
+            lat_tile(i, 2)
             evac_s(i, 2)
+            rope_evac(i)
             evac_v(i, 2)
             mulx(i + 1, 1)
             kv_mm(i - 1, 0)
@@ -344,18 +361,19 @@ def tile_gptossmlaattention_pa_t_kernel(tc, x_bytes, x_scale, cos, sin, wkva, bk
             lat_tile(i, 3)
             kv_mm(i - 1, 1)
             kv_evac(i - 1, 1)
+            store_k1(i - 1)
             inter(i)
+            rope_trans(i)
             trans(i + 2, 0)
             trans(i + 2, 1)
             quant_x(i + 1)
             evac_v(i, 3)
             rope(i - 1)
             kv_mm(i - 1, 2)
+            bias_rope(i)
             kv_evac(i - 1, 2)
             store_v(i - 1)
             cast(i + 3, 0)
             cast(i + 3, 1)
-            bias_rope(i)
             quant_l(i)
-            dup(i - 1)
             store_kk(i - 1)

@@ -17,6 +17,7 @@ IDENT = mybir.ActivationFunctionType.Identity
 P = 128
 S, K, R = 8192, 512, 512
 ROPE, NOPE, VD, NH = 128, 64, 128, 2
+HALF = ROPE // 2
 TPP = S // P
 TB = 4
 NB = TPP // TB
@@ -30,9 +31,9 @@ def tile_gptossmlaattention_pa_t_kernel(tc, x_bytes, x_scale, cos, sin, wkva, bk
     with ExitStack() as ctx:
         ctx.enter_context(tc.manual_schedule())
         keep = ctx.enter_context(tc.tile_pool(name="keep", bufs=1))
-        xin = ctx.enter_context(tc.tile_pool(name="xin", bufs=1))
         p2 = ctx.enter_context(tc.tile_pool(name="p2", bufs=2))
         p3 = ctx.enter_context(tc.tile_pool(name="p3", bufs=3))
+        plg = ctx.enter_context(tc.tile_pool(name="plg", bufs=1))
         outp = ctx.enter_context(tc.tile_pool(name="outp", bufs=4))
         ps_x = ctx.enter_context(tc.psum_pool(name="ps_x", bufs=2))
         ps_l = ctx.enter_context(tc.psum_pool(name="ps_l", bufs=3))
@@ -46,13 +47,11 @@ def tile_gptossmlaattention_pa_t_kernel(tc, x_bytes, x_scale, cos, sin, wkva, bk
         kk1_rows = kk_out[:, 1].rearrange("o (p s) c -> p (o s) c", p=P)
         v_rows = v_out.rearrange("o h (p s) c -> p (o h) (s c)", p=P)
 
-        x_sb = []
-        c_sb = []
-        s_sb = []
+        x_sb, c_sb, s_sb = [], [], []
         for g in range(TPP // CHUNK):
-            xt = xin.tile([P, CHUNK * K], U8, name="x%d" % g)
-            ct = xin.tile([P, CHUNK * ROPE], BF16, name="c%d" % g)
-            st = xin.tile([P, CHUNK * ROPE], BF16, name="s%d" % g)
+            xt = keep.tile([P, CHUNK * K], U8, name="x%d" % g)
+            ct = keep.tile([P, CHUNK * ROPE], BF16, name="c%d" % g)
+            st = keep.tile([P, CHUNK * ROPE], BF16, name="s%d" % g)
             x_sb.append(xt)
             c_sb.append(ct)
             s_sb.append(st)
@@ -70,7 +69,8 @@ def tile_gptossmlaattention_pa_t_kernel(tc, x_bytes, x_scale, cos, sin, wkva, bk
         scale = keep.tile([P, 4], F32, name="scale")
         bias_l = keep.tile([P, 4], BF16, name="bias_l")
         bias_r = keep.tile([P, 1], BF16, name="bias_r")
-        load_x(0, 0, 4)
+        load_x(0, 0, 2)
+        load_x(0, 2, 4)
         nc.sync.dma_start(out=wa_raw[:], in_=wkva.rearrange("(p j) w -> p j w", j=4))
         nc.sync.dma_start(out=scale[:], in_=x_scale.rearrange("a b (p t) -> p (a b t)", t=4))
         nc.sync.dma_start(out=bias_l[:], in_=bkva[0:R].rearrange("(p t) -> p t", t=4))
@@ -82,11 +82,11 @@ def tile_gptossmlaattention_pa_t_kernel(tc, x_bytes, x_scale, cos, sin, wkva, bk
             load_x(g, 0, CHUNK)
             load_cs(g)
 
-        ident = keep.tile([P, P], F32, name="ident")
-        make_identity(nc, ident[:])
         warm = keep.tile([P, 1], F32, name="warm")
         nc.vector.memset(warm[:], 0.0)
         nc.scalar.activation(out=warm[:], in_=warm[:], func=IDENT)
+        ident = keep.tile([P, P], F32, name="ident")
+        make_identity(nc, ident[:])
 
         wa_g = keep.tile([P, R * 4], BF16, align_bytes=64, name="wa_g")
         wr_g = keep.tile([P, ROPE * 4], BF16, align_bytes=64, name="wr_g")
@@ -107,23 +107,30 @@ def tile_gptossmlaattention_pa_t_kernel(tc, x_bytes, x_scale, cos, sin, wkva, bk
         def prep_wa():
             src = wa_raw[:, :, 0:R].rearrange("p j (m t) -> p t m j", t=4)
             dst = wa_g[:].rearrange("p (t m j) -> p t m j", t=4, j=4)
-            for t in range(4):
+            for t in range(2):
                 nc.vector.tensor_copy(out=dst[:, t], in_=src[:, t])
-            nc.vector.tensor_copy(out=wr_g[:].rearrange("p (c j) -> p c j", j=4), in_=wa_raw[:, :, R:].rearrange("p j c -> p c j"))
+                nc.scalar.copy(out=dst[:, t + 2], in_=src[:, t + 2])
+            nc.scalar.copy(out=wr_g[:].rearrange("p (c j) -> p c j", j=4), in_=wa_raw[:, :, R:].rearrange("p j c -> p c j"))
+
+        def quant_wa():
             quant(wa_c[:], wa_s[:], wa_g[:])
             quant(wr_c[:], wr_s[:], wr_g[:])
 
         def prep_wb():
             src = wb_raw[:].rearrange("p j (h w) -> p h w j", h=NH)
             for h in range(NH):
-                nc.vector.tensor_copy(out=wn_g[:].rearrange("p (h c j) -> p h c j", h=NH, j=4)[:, h], in_=src[:, h, 0:NOPE])
-                nc.vector.tensor_copy(out=wv_g[:].rearrange("p (h c j) -> p h c j", h=NH, j=4)[:, h], in_=src[:, h, NOPE:])
+                nc.gpsimd.tensor_scalar(out=wn_g[:].rearrange("p (h c j) -> p h c j", h=NH, j=4)[:, h], in0=src[:, h, 0:NOPE],
+                                        scalar1=1.0, scalar2=0.0, op0=MULT, op1=ADD)
+                nc.gpsimd.tensor_scalar(out=wv_g[:].rearrange("p (h c j) -> p h c j", h=NH, j=4)[:, h], in0=src[:, h, NOPE:],
+                                        scalar1=1.0, scalar2=0.0, op0=MULT, op1=ADD)
+
+        def quant_wb():
             quant(wn_c[:], wn_s[:], wn_g[:])
             quant(wv_c[:], wv_s[:], wv_g[:])
 
         xw, xps, xg, xc, xs = {}, {}, {}, {}, {}
         lps, lpl, lg, lc, ls = {}, {}, {}, {}, {}
-        rps, kt, krb, kvps, kk, vt = {}, {}, {}, {}, {}, {}
+        rps, kt, m1, m2, kvps, kk, vt = {}, {}, {}, {}, {}, {}, {}
 
         def ok(b):
             return 0 <= b < NB
@@ -168,8 +175,8 @@ def tile_gptossmlaattention_pa_t_kernel(tc, x_bytes, x_scale, cos, sin, wkva, bk
         def quant_x(b):
             if not ok(b):
                 return
-            t_xc = p3.tile([P, TB * P], U32, align_bytes=64, name="t_xc")
-            t_xs = p3.tile([P, TB * P], U8, align_bytes=64, name="t_xs")
+            t_xc = p2.tile([P, TB * P], U32, align_bytes=64, name="t_xc")
+            t_xs = p2.tile([P, TB * P], U8, align_bytes=64, name="t_xs")
             xc[b], xs[b] = t_xc, t_xs
             quant(t_xc[:], t_xs[:], xg[b][:])
 
@@ -221,25 +228,58 @@ def tile_gptossmlaattention_pa_t_kernel(tc, x_bytes, x_scale, cos, sin, wkva, bk
                 n = slice(j * P, (j + 1) * P)
                 nc.tensor.transpose(t_rps[:, n], kt[b][:, n], ident[:])
 
+        def cs(b, tiles):
+            g, o = divmod(b * TB, CHUNK)
+            return tiles[g][:].rearrange("p (s c) -> p s c", c=ROPE)[:, o : o + TB, :]
+
+        def rope_mul(b):
+            if not ok(b):
+                return
+            t_m1 = p2.tile([P, TB, ROPE], F32, name="t_m1")
+            t_m2 = p2.tile([P, TB, ROPE], F32, name="t_m2")
+            m1[b], m2[b] = t_m1, t_m2
+            k = rps[b][:].rearrange("p (j c) -> p j c", c=ROPE)
+            c, s = cs(b, c_sb), cs(b, s_sb)
+            nc.vector.tensor_tensor(out=t_m1[:], in0=k, in1=c, op=MULT)
+            nc.vector.tensor_tensor(out=t_m2[:, :, 0:HALF], in0=k[:, :, HALF:], in1=s[:, :, 0:HALF], op=MULT)
+            nc.vector.tensor_tensor(out=t_m2[:, :, HALF:], in0=k[:, :, 0:HALF], in1=s[:, :, HALF:], op=MULT)
+
+        def rope_add(b):
+            if not ok(b):
+                return
+            nc.gpsimd.tensor_tensor(out=kk[b][:, 0, :, NOPE : NOPE + HALF], in0=m1[b][:, :, 0:HALF], in1=m2[b][:, :, 0:HALF], op=SUB)
+            nc.gpsimd.tensor_tensor(out=kk[b][:, 0, :, NOPE + HALF :], in0=m1[b][:, :, HALF:], in1=m2[b][:, :, HALF:], op=ADD)
+
         def evac_s(b, t0):
             if not ok(b):
                 return
             if t0 == 0:
-                t_lpl = p2.tile([P, 4, 2 * P], BF16, align_bytes=64, name="t_lpl")
+                t_lpl = p2.tile([P, 4, 3 * P], BF16, align_bytes=64, name="t_lpl")
                 lpl[b] = t_lpl
             for t in (t0, t0 + 1):
-                nc.scalar.activation(out=lpl[b][:, t, :], in_=lps[b, "s", t0][:, t - t0, :], func=IDENT, bias=bias_l[:, t : t + 1])
+                nc.scalar.activation(out=lpl[b][:, t, 0 : 2 * P], in_=lps[b, "s", t0][:, t - t0, :], func=IDENT, bias=bias_l[:, t : t + 1])
+
+        def evac_s1(b, j):
+            if not ok(b):
+                return
+            for t in range(4):
+                nc.scalar.activation(out=lpl[b][:, t, j * P : (j + 1) * P], in_=lps[b, "v", j][:, t, :], func=IDENT, bias=bias_l[:, t : t + 1])
 
         def new_lg(b):
             if not ok(b):
                 return
-            t_lg = p2.tile([P, TB * P * 4], BF16, align_bytes=64, name="t_lg")
+            t_lg = plg.tile([P, TB * P * 4], BF16, align_bytes=64, name="t_lg")
             lg[b] = t_lg
 
-        def inter(b):
+        def inter(b, j, eng):
             if not ok(b):
                 return
-            nc.vector.tensor_copy(out=lg[b][:, 0:1024].rearrange("p (n t) -> p n t", t=4), in_=lpl[b][:].rearrange("p t n -> p n t"))
+            dst = lg[b][:, j * 512 : (j + 1) * 512].rearrange("p (n t) -> p n t", t=4)
+            src = lpl[b][:, :, j * P : (j + 1) * P].rearrange("p t n -> p n t")
+            if eng == "g":
+                nc.gpsimd.tensor_scalar(out=dst, in0=src, scalar1=1.0, scalar2=0.0, op0=MULT, op1=ADD)
+            else:
+                nc.vector.tensor_copy(out=dst, in_=src)
 
         def evac_v(b, j):
             if not ok(b):
@@ -248,13 +288,6 @@ def tile_gptossmlaattention_pa_t_kernel(tc, x_bytes, x_scale, cos, sin, wkva, bk
                 out=lg[b][:, j * 512 : (j + 1) * 512].rearrange("p (n t) -> p n t", t=4),
                 in0=lps[b, "v", j][:].rearrange("p t n -> p n t"),
                 in1=bias_l[:].unsqueeze(1).to_broadcast([P, P, 4]), op=ADD)
-
-        def bias_rope(b):
-            if not ok(b):
-                return
-            t_krb = p2.tile([P, TB, ROPE], F32, name="t_krb")
-            krb[b] = t_krb
-            nc.scalar.copy(out=t_krb[:].rearrange("p j c -> p (j c)"), in_=rps[b][:])
 
         def quant_l(b):
             if not ok(b):
@@ -277,7 +310,7 @@ def tile_gptossmlaattention_pa_t_kernel(tc, x_bytes, x_scale, cos, sin, wkva, bk
                     out=t_kv[:, i * width : (i + 1) * width], lhsT=lc[b][:, n].bitcast(FP8X4), lhsT_scale=ls[b][:, n],
                     rhs=wc[:].bitcast(FP8X4), rhs_scale=ws[:], start=True, stop=True)
 
-        def new_out(b):
+        def new_kk(b):
             if not ok(b):
                 return
             t_kk = outp.tile([P, NH, TB, NOPE + ROPE], F32, name="t_kk")
@@ -294,36 +327,24 @@ def tile_gptossmlaattention_pa_t_kernel(tc, x_bytes, x_scale, cos, sin, wkva, bk
                 nc.scalar.copy(out=vt[b][:, :, 2 * part - 2 : 2 * part, :].rearrange("p h j c -> p j h c"),
                                in_=kvps[b, part][:].rearrange("p (j h c) -> p j h c", j=2, h=NH))
 
-        def rope(b):
-            if not ok(b):
-                return
-            g, o = divmod(b * TB, CHUNK)
-            c = c_sb[g][:].rearrange("p (s c) -> p s c", c=ROPE)[:, o : o + TB, :]
-            s = s_sb[g][:].rearrange("p (s c) -> p s c", c=ROPE)[:, o : o + TB, :]
-            m1 = p2.tile([P, TB, ROPE], F32, name="m1")
-            m2 = p2.tile([P, TB, ROPE], F32, name="m2")
-            k = krb[b]
-            hf = ROPE // 2
-            nc.gpsimd.tensor_tensor(out=m1[:], in0=k[:], in1=c, op=MULT)
-            nc.gpsimd.tensor_tensor(out=m2[:, :, 0:hf], in0=k[:, :, hf:], in1=s[:, :, 0:hf], op=MULT)
-            nc.gpsimd.tensor_tensor(out=m2[:, :, hf:], in0=k[:, :, 0:hf], in1=s[:, :, hf:], op=MULT)
-            nc.gpsimd.tensor_tensor(out=kk[b][:, 0, :, NOPE : NOPE + hf], in0=m1[:, :, 0:hf], in1=m2[:, :, 0:hf], op=SUB)
-            nc.gpsimd.tensor_tensor(out=kk[b][:, 0, :, NOPE + hf :], in0=m1[:, :, hf:], in1=m2[:, :, hf:], op=ADD)
-
         def store_v(b):
             if not ok(b):
                 return
             w = TB * VD
             nc.sync.dma_start(out=v_rows[:, :, b * w : (b + 1) * w], in_=vt[b][:].rearrange("p h j c -> p h (j c)"))
 
-        def store_kk(b):
+        def store_k0(b):
             if not ok(b):
                 return
             w = TB * (NOPE + ROPE)
             nc.sync.dma_start(out=kk_rows[:, 0, b * w : (b + 1) * w], in_=kk[b][:, 0].rearrange("p j c -> p (j c)"))
+
+        def store_r1(b):
+            if not ok(b):
+                return
             nc.sync.dma_start(out=kk1_rows[:, b * TB : (b + 1) * TB, NOPE:], in_=kk[b][:, 0, :, NOPE:])
 
-        def store_k1(b):
+        def store_n1(b):
             if not ok(b):
                 return
             nc.sync.dma_start(out=kk1_rows[:, b * TB : (b + 1) * TB, 0:NOPE], in_=kk[b][:, 1, :, 0:NOPE])
@@ -333,47 +354,68 @@ def tile_gptossmlaattention_pa_t_kernel(tc, x_bytes, x_scale, cos, sin, wkva, bk
         trans(0, 0)
         trans(0, 1)
         prep_wa()
+        prep_wb()
         cast(1, 0)
         cast(1, 1)
         mulx(0, 0)
         mulx(0, 1)
+        quant_wa()
         trans(1, 0)
         trans(1, 1)
         cast(2, 0)
         cast(2, 1)
         quant_x(0)
-        prep_wb()
-        for i in range(NB + 2):
-            new_lg(i)
-            new_out(i - 1)
-            lat_pair(i, 0)
-            lat_pair(i, 2)
-            evac_s(i, 0)
-            mulx(i + 1, 0)
-            rope_mm(i)
-            lat_tile(i, 2)
-            evac_s(i, 2)
-            rope_evac(i)
-            evac_v(i, 2)
-            mulx(i + 1, 1)
-            kv_mm(i - 1, 0)
-            kv_evac(i - 1, 0)
-            lat_tile(i, 3)
-            kv_mm(i - 1, 1)
-            kv_evac(i - 1, 1)
-            store_k1(i - 1)
-            inter(i)
-            rope_trans(i)
-            trans(i + 2, 0)
-            trans(i + 2, 1)
+        mulx(1, 0)
+        mulx(1, 1)
+        lat_pair(0, 0)
+        lat_pair(0, 2)
+        evac_s(0, 0)
+        rope_mm(0)
+        lat_tile(0, 2)
+        evac_s(0, 2)
+        rope_evac(0)
+        lat_tile(0, 3)
+        evac_s1(0, 2)
+        trans(2, 0)
+        trans(2, 1)
+        rope_trans(0)
+        cast(3, 0)
+        cast(3, 1)
+        quant_wb()
+        for i in range(NB + 1):
+            new_kk(i)
             quant_x(i + 1)
-            evac_v(i, 3)
-            rope(i - 1)
+            quant_l(i - 1)
+            kv_mm(i - 1, 0)
+            lat_pair(i + 1, 0)
+            kv_mm(i - 1, 1)
+            lat_pair(i + 1, 2)
+            new_lg(i)
+            evac_s(i + 1, 0)
+            kv_evac(i - 1, 0)
+            store_n1(i - 1)
+            inter(i, 0, "g")
+            inter(i, 1, "g")
+            inter(i, 2, "g")
+            mulx(i + 2, 0)
+            evac_s(i + 1, 2)
+            rope_mul(i)
+            kv_evac(i - 1, 1)
+            rope_mm(i + 1)
+            lat_tile(i + 1, 2)
             kv_mm(i - 1, 2)
-            bias_rope(i)
+            rope_evac(i + 1)
+            evac_s1(i + 1, 2)
+            mulx(i + 2, 1)
+            rope_add(i)
             kv_evac(i - 1, 2)
             store_v(i - 1)
-            cast(i + 3, 0)
-            cast(i + 3, 1)
-            quant_l(i)
-            store_kk(i - 1)
+            evac_v(i, 3)
+            lat_tile(i + 1, 3)
+            rope_trans(i + 1)
+            trans(i + 3, 0)
+            trans(i + 3, 1)
+            cast(i + 4, 0)
+            cast(i + 4, 1)
+            store_k0(i - 1)
+            store_r1(i - 1)

@@ -22,6 +22,7 @@ TPP = S // P
 TB = 4
 NB = TPP // TB
 CHUNK = 8
+WV = 512
 
 FLOPS = 2 * S * K * (R + ROPE) + 2 * S * R * NH * (NOPE + VD)
 
@@ -70,18 +71,19 @@ def tile_gptossmlaattention_pa_t_kernel(tc, x_bytes, x_scale, cos, sin, wkva, bk
         bias_l = keep.tile([P, 4], BF16, name="bias_l")
         bias_r = keep.tile([P, 1], BF16, name="bias_r")
         load_x(0, 0, 2)
+        nc.sync.dma_start(out=scale[:], in_=x_scale.rearrange("a b (p t) -> p (a b t)", t=4))
         load_x(0, 2, 4)
         nc.sync.dma_start(out=wa_raw[:], in_=wkva.rearrange("(p j) w -> p j w", j=4))
-        nc.sync.dma_start(out=scale[:], in_=x_scale.rearrange("a b (p t) -> p (a b t)", t=4))
+        load_x(0, 4, 8)
         nc.sync.dma_start(out=bias_l[:], in_=bkva[0:R].rearrange("(p t) -> p t", t=4))
         nc.sync.dma_start(out=bias_r[:], in_=bkva[R : R + ROPE].rearrange("(p o) -> p o", o=1))
-        load_x(0, 4, 8)
-        nc.sync.dma_start(out=wb_raw[:], in_=wkvb.rearrange("(p j) w -> p j w", j=4))
+        load_x(1, 0, CHUNK)
         load_cs(0)
-        for g in range(1, TPP // CHUNK):
+        nc.sync.dma_start(out=wb_raw[:], in_=wkvb.rearrange("(p j) w -> p j w", j=4))
+        load_cs(1)
+        for g in range(2, TPP // CHUNK):
             load_x(g, 0, CHUNK)
             load_cs(g)
-
         warm = keep.tile([P, 1], F32, name="warm")
         nc.vector.memset(warm[:], 0.0)
         nc.scalar.activation(out=warm[:], in_=warm[:], func=IDENT)
@@ -104,16 +106,20 @@ def tile_gptossmlaattention_pa_t_kernel(tc, x_bytes, x_scale, cos, sin, wkva, bk
         def quant(codes, scales, src):
             nc.vector.quantize_mx(out=codes.bitcast(FP8X4), scales=scales, in_=src)
 
-        def prep_wa():
+        def prep_wa(t, eng):
             src = wa_raw[:, :, 0:R].rearrange("p j (m t) -> p t m j", t=4)
             dst = wa_g[:].rearrange("p (t m j) -> p t m j", t=4, j=4)
-            for t in range(2):
-                nc.vector.tensor_copy(out=dst[:, t], in_=src[:, t])
-                nc.scalar.copy(out=dst[:, t + 2], in_=src[:, t + 2])
-            nc.scalar.copy(out=wr_g[:].rearrange("p (c j) -> p c j", j=4), in_=wa_raw[:, :, R:].rearrange("p j c -> p c j"))
+            copy = nc.scalar.copy if eng == "s" else nc.vector.tensor_copy
+            copy(out=dst[:, t], in_=src[:, t])
+
+        def prep_wr():
+            nc.gpsimd.tensor_scalar(out=wr_g[:].rearrange("p (c j) -> p c j", j=4), in0=wa_raw[:, :, R:].rearrange("p j c -> p c j"),
+                                    scalar1=1.0, scalar2=0.0, op0=MULT, op1=ADD)
 
         def quant_wa():
             quant(wa_c[:], wa_s[:], wa_g[:])
+
+        def quant_wr():
             quant(wr_c[:], wr_s[:], wr_g[:])
 
         def prep_wb():
@@ -128,23 +134,23 @@ def tile_gptossmlaattention_pa_t_kernel(tc, x_bytes, x_scale, cos, sin, wkva, bk
             quant(wn_c[:], wn_s[:], wn_g[:])
             quant(wv_c[:], wv_s[:], wv_g[:])
 
-        xw, xps, xg, xc, xs = {}, {}, {}, {}, {}
+        qt, qc, xw, xps, xg, xc, xs = {}, {}, {}, {}, {}, {}, {}
         lps, lpl, lg, lc, ls = {}, {}, {}, {}, {}
         rps, kt, m1, m2, kvps, kk, vt = {}, {}, {}, {}, {}, {}, {}
 
         def ok(b):
             return 0 <= b < NB
 
-        def cast(b, h):
+        def cast(b, c0, c1, eng):
             if not ok(b):
                 return
-            if h == 0:
+            if c0 == 0:
                 t_xw = p3.tile([P, TB, K], BF16, align_bytes=64, name="t_xw")
                 xw[b] = t_xw
-            g, o = divmod(b * TB + 2 * h, CHUNK)
-            src = x_sb[g][:, o * K : (o + 2) * K].bitcast(FP8)
-            dst = xw[b][:, 2 * h : 2 * h + 2, :].rearrange("p j k -> p (j k)")
-            if b == 0:
+            g, o = divmod(b * TB, CHUNK)
+            src = x_sb[g][:, o * K + c0 : o * K + c1].bitcast(FP8)
+            dst = xw[b][:].rearrange("p j k -> p (j k)")[:, c0:c1]
+            if eng == "v":
                 nc.vector.tensor_copy(out=dst, in_=src)
             else:
                 nc.scalar.copy(out=dst, in_=src)
@@ -162,9 +168,6 @@ def tile_gptossmlaattention_pa_t_kernel(tc, x_bytes, x_scale, cos, sin, wkva, bk
         def mulx(b, h):
             if not ok(b):
                 return
-            if h == 0:
-                t_xg = p2.tile([P, TB * P * 4], BF16, align_bytes=64, name="t_xg")
-                xg[b] = t_xg
             nc.vector.tensor_tensor(
                 out=xg[b][:, h * 1024 : (h + 1) * 1024].rearrange("p (c u e) -> p c u e", u=2, e=2),
                 in0=xps[b, h][:].bitcast(BF16).rearrange("p u (c e) -> p c u e", e=2),
@@ -172,13 +175,31 @@ def tile_gptossmlaattention_pa_t_kernel(tc, x_bytes, x_scale, cos, sin, wkva, bk
                 op=MULT,
             )
 
-        def quant_x(b):
-            if not ok(b):
-                return
-            t_xc = p2.tile([P, TB * P], U32, align_bytes=64, name="t_xc")
-            t_xs = p2.tile([P, TB * P], U8, align_bytes=64, name="t_xs")
-            xc[b], xs[b] = t_xc, t_xs
-            quant(t_xc[:], t_xs[:], xg[b][:])
+        W4 = TB * P * 4
+
+        def new_q(i):
+            t_q = plg.tile([P, 2 * W4], BF16, align_bytes=64, name="t_q")
+            qt[i] = t_q
+            xg[i + 1], lg[i - 1] = t_q[:, 0:W4], t_q[:, W4:]
+
+        def quant_q(i, part="xl"):
+            n = TB * P
+            if "x" in part or i + 1 >= NB:
+                t_qc = p2.tile([P, 2 * TB * P], U32, align_bytes=64, name="t_qc")
+                t_qs = p2.tile([P, 2 * TB * P], U8, align_bytes=64, name="t_qs")
+                qc[i] = t_qc, t_qs
+            t_qc, t_qs = qc[i]
+            xc[i + 1], xs[i + 1] = t_qc[:, 0:n], t_qs[:, 0:n]
+            lc[i - 1], ls[i - 1] = t_qc[:, n:], t_qs[:, n:]
+            lo = 0 if ok(i + 1) and "x" in part else n
+            hi = 2 * n if ok(i - 1) and "l" in part else n
+            quant(t_qc[:, lo:hi], t_qs[:, lo:hi], qt[i][:, 4 * lo : 4 * hi])
+
+        def quant_last(i, h):
+            n = TB * P // 2
+            t_qc, t_qs = qc[i]
+            lc[i], ls[i] = t_qc[:, 0 : 2 * n], t_qs[:, 0 : 2 * n]
+            quant(t_qc[:, h * n : (h + 1) * n], t_qs[:, h * n : (h + 1) * n], qt[i][:, 4 * h * n : 4 * (h + 1) * n])
 
         def lat_pair(b, t0):
             if not ok(b):
@@ -210,7 +231,7 @@ def tile_gptossmlaattention_pa_t_kernel(tc, x_bytes, x_scale, cos, sin, wkva, bk
             rps[b] = t_rps
             nc.tensor.matmul_mx(
                 out=t_rps[:], lhsT=wr_c[:].bitcast(FP8X4), lhsT_scale=wr_s[:],
-                rhs=xc[b][:].bitcast(FP8X4), rhs_scale=xs[b][:], start=True, stop=True)
+                rhs=xc[b].bitcast(FP8X4), rhs_scale=xs[b], start=True, stop=True)
 
         def rope_evac(b):
             if not ok(b):
@@ -241,8 +262,8 @@ def tile_gptossmlaattention_pa_t_kernel(tc, x_bytes, x_scale, cos, sin, wkva, bk
             k = rps[b][:].rearrange("p (j c) -> p j c", c=ROPE)
             c, s = cs(b, c_sb), cs(b, s_sb)
             nc.vector.tensor_tensor(out=t_m1[:], in0=k, in1=c, op=MULT)
-            nc.vector.tensor_tensor(out=t_m2[:, :, 0:HALF], in0=k[:, :, HALF:], in1=s[:, :, 0:HALF], op=MULT)
-            nc.vector.tensor_tensor(out=t_m2[:, :, HALF:], in0=k[:, :, 0:HALF], in1=s[:, :, HALF:], op=MULT)
+            nc.vector.tensor_tensor(out=t_m2[:].rearrange("p j (h c) -> p j h c", h=2), in0=k.rearrange("p j (h c) -> p j h c", h=2)[:, :, ::-1, :],
+                                    in1=s.rearrange("p j (h c) -> p j h c", h=2), op=MULT)
 
         def rope_add(b):
             if not ok(b):
@@ -265,12 +286,6 @@ def tile_gptossmlaattention_pa_t_kernel(tc, x_bytes, x_scale, cos, sin, wkva, bk
             for t in range(4):
                 nc.scalar.activation(out=lpl[b][:, t, j * P : (j + 1) * P], in_=lps[b, "v", j][:, t, :], func=IDENT, bias=bias_l[:, t : t + 1])
 
-        def new_lg(b):
-            if not ok(b):
-                return
-            t_lg = plg.tile([P, TB * P * 4], BF16, align_bytes=64, name="t_lg")
-            lg[b] = t_lg
-
         def inter(b, j, eng):
             if not ok(b):
                 return
@@ -289,14 +304,6 @@ def tile_gptossmlaattention_pa_t_kernel(tc, x_bytes, x_scale, cos, sin, wkva, bk
                 in0=lps[b, "v", j][:].rearrange("p t n -> p n t"),
                 in1=bias_l[:].unsqueeze(1).to_broadcast([P, P, 4]), op=ADD)
 
-        def quant_l(b):
-            if not ok(b):
-                return
-            t_lc = p2.tile([P, TB * P], U32, align_bytes=64, name="t_lc")
-            t_ls = p2.tile([P, TB * P], U8, align_bytes=64, name="t_ls")
-            lc[b], ls[b] = t_lc, t_ls
-            quant(t_lc[:], t_ls[:], lg[b][:])
-
         def kv_mm(b, part):
             if not ok(b):
                 return
@@ -310,6 +317,32 @@ def tile_gptossmlaattention_pa_t_kernel(tc, x_bytes, x_scale, cos, sin, wkva, bk
                     out=t_kv[:, i * width : (i + 1) * width], lhsT=lc[b][:, n].bitcast(FP8X4), lhsT_scale=ls[b][:, n],
                     rhs=wc[:].bitcast(FP8X4), rhs_scale=ws[:], start=True, stop=True)
 
+        def kv_half(b, h):
+            t_kn = ps_kv.tile([P, 512], F32, name="t_kv")
+            t_kv = ps_kv.tile([P, 512], F32, name="t_kv")
+            kvps[b, "n", h], kvps[b, h + 1] = t_kn, t_kv
+            for dst, wc, ws, width in ((t_kn, wn_c, wn_s, 128), (t_kv, wv_c, wv_s, 256)):
+                for i in range(2):
+                    n = slice((2 * h + i) * P, (2 * h + i + 1) * P)
+                    nc.tensor.matmul_mx(
+                        out=dst[:, i * width : (i + 1) * width], lhsT=lc[b][:, n].bitcast(FP8X4), lhsT_scale=ls[b][:, n],
+                        rhs=wc[:].bitcast(FP8X4), rhs_scale=ws[:], start=True, stop=True)
+
+        def nope_half(b, h, eng):
+            copy = nc.scalar.copy if eng == "s" else nc.vector.tensor_copy
+            copy(out=kk[b][:, :, 2 * h : 2 * h + 2, 0:NOPE].rearrange("p h j c -> p j h c"),
+                 in_=kvps[b, "n", h][:, 0 : 2 * P].rearrange("p (j h c) -> p j h c", j=2, h=NH))
+
+        def store_half(b, h):
+            w = 2 * (NOPE + ROPE)
+            o = b * 2 * w + h * w
+            nc.sync.dma_start(out=kk_rows[:, :, o : o + w], in_=kk[b][:, :, 2 * h : 2 * h + 2, :].rearrange("p h j c -> p h (j c)"))
+
+        def storev_half(b, h):
+            w = 2 * VD
+            o = b * 2 * w + h * w
+            nc.sync.dma_start(out=v_rows[:, :, o : o + w], in_=vt[b][:, :, 2 * h : 2 * h + 2, :].rearrange("p h j c -> p h (j c)"))
+
         def new_kk(b):
             if not ok(b):
                 return
@@ -317,15 +350,23 @@ def tile_gptossmlaattention_pa_t_kernel(tc, x_bytes, x_scale, cos, sin, wkva, bk
             t_v = outp.tile([P, NH, TB, VD], F32, name="t_v")
             kk[b], vt[b] = t_kk, t_v
 
-        def kv_evac(b, part):
+        def kv_evac(b, part, eng="s"):
             if not ok(b):
                 return
+            copy = nc.scalar.copy if eng == "s" else nc.vector.tensor_copy
             if part == 0:
-                nc.scalar.copy(out=kk[b][:, :, :, 0:NOPE].rearrange("p h j c -> p j h c"),
-                               in_=kvps[b, 0][:].rearrange("p (j h c) -> p j h c", j=TB, h=NH))
+                copy(out=kk[b][:, :, :, 0:NOPE].rearrange("p h j c -> p j h c"),
+                     in_=kvps[b, 0][:].rearrange("p (j h c) -> p j h c", j=TB, h=NH))
             else:
-                nc.scalar.copy(out=vt[b][:, :, 2 * part - 2 : 2 * part, :].rearrange("p h j c -> p j h c"),
-                               in_=kvps[b, part][:].rearrange("p (j h c) -> p j h c", j=2, h=NH))
+                copy(out=vt[b][:, :, 2 * part - 2 : 2 * part, :].rearrange("p h j c -> p j h c"),
+                     in_=kvps[b, part][:].rearrange("p (j h c) -> p j h c", j=2, h=NH))
+
+        def dup_v(b):
+            nc.gpsimd.tensor_scalar(out=kk[b][:, 1, :, NOPE:], in0=kk[b][:, 0, :, NOPE:], scalar1=1.0, scalar2=0.0, op0=MULT, op1=ADD)
+
+        def store_k01(b):
+            w = TB * (NOPE + ROPE)
+            nc.sync.dma_start(out=kk_rows[:, :, b * w : (b + 1) * w], in_=kk[b][:].rearrange("p h j c -> p h (j c)"))
 
         def store_v(b):
             if not ok(b):
@@ -349,73 +390,148 @@ def tile_gptossmlaattention_pa_t_kernel(tc, x_bytes, x_scale, cos, sin, wkva, bk
                 return
             nc.sync.dma_start(out=kk1_rows[:, b * TB : (b + 1) * TB, 0:NOPE], in_=kk[b][:, 1, :, 0:NOPE])
 
-        cast(0, 0)
-        cast(0, 1)
+        def casts(b):
+            cast(b, 0, 1024, "s")
+            cast(b, 1024, 2048 - WV, "s")
+
+        def cast_v(b):
+            cast(b, 2048 - WV, 2048, "v")
+
+        new_q(-1)
+        cast(0, 0, 1024, "v")
+        cast(0, 1024, 2048, "s")
         trans(0, 0)
         trans(0, 1)
-        prep_wa()
-        prep_wb()
-        cast(1, 0)
-        cast(1, 1)
         mulx(0, 0)
+        prep_wr()
+        prep_wa(1, "s")
+        prep_wa(2, "s")
+        prep_wa(3, "s")
         mulx(0, 1)
+        prep_wa(0, "v")
+        casts(1)
+        quant_q(-1)
         quant_wa()
+        cast_v(1)
+        quant_wr()
         trans(1, 0)
         trans(1, 1)
-        cast(2, 0)
-        cast(2, 1)
-        quant_x(0)
+        new_q(0)
         mulx(1, 0)
-        mulx(1, 1)
+        rope_mm(0)
         lat_pair(0, 0)
         lat_pair(0, 2)
-        evac_s(0, 0)
-        rope_mm(0)
-        lat_tile(0, 2)
-        evac_s(0, 2)
         rope_evac(0)
+        evac_s(0, 0)
+        lat_tile(0, 2)
+        rope_trans(0)
+        evac_s(0, 2)
+        mulx(1, 1)
+        prep_wb()
         lat_tile(0, 3)
+        casts(2)
         evac_s1(0, 2)
+        cast_v(2)
         trans(2, 0)
         trans(2, 1)
-        rope_trans(0)
-        cast(3, 0)
-        cast(3, 1)
-        quant_wb()
-        for i in range(NB + 1):
+        casts(3)
+        for i in range(NB - 2):
             new_kk(i)
-            quant_x(i + 1)
-            quant_l(i - 1)
-            kv_mm(i - 1, 0)
+            cast_v(i + 3)
+            quant_q(i)
             lat_pair(i + 1, 0)
             kv_mm(i - 1, 1)
+            kv_mm(i - 1, 0)
             lat_pair(i + 1, 2)
-            new_lg(i)
+            new_q(i + 1)
             evac_s(i + 1, 0)
-            kv_evac(i - 1, 0)
-            store_n1(i - 1)
             inter(i, 0, "g")
             inter(i, 1, "g")
             inter(i, 2, "g")
-            mulx(i + 2, 0)
-            evac_s(i + 1, 2)
+            kv_evac(i - 1, 0)
             rope_mul(i)
-            kv_evac(i - 1, 1)
+            evac_s(i + 1, 2)
+            mulx(i + 2, 0)
+            rope_add(i)
             rope_mm(i + 1)
+            store_n1(i - 1)
             lat_tile(i + 1, 2)
             kv_mm(i - 1, 2)
+            kv_evac(i - 1, 1)
             rope_evac(i + 1)
             evac_s1(i + 1, 2)
-            mulx(i + 2, 1)
-            rope_add(i)
+            evac_v(i, 3)
             kv_evac(i - 1, 2)
             store_v(i - 1)
-            evac_v(i, 3)
-            lat_tile(i + 1, 3)
-            rope_trans(i + 1)
+            mulx(i + 2, 1)
+            if i == 0:
+                quant_wb()
             trans(i + 3, 0)
+            rope_trans(i + 1)
             trans(i + 3, 1)
-            cast(i + 4, 0)
-            cast(i + 4, 1)
+            casts(i + 4)
             store_k0(i - 1)
+            lat_tile(i + 1, 3)
             store_r1(i - 1)
+        a, z = NB - 2, NB - 1
+        new_kk(a)
+        new_kk(z)
+        quant_q(a, "x")
+        lat_pair(z, 0)
+        lat_pair(z, 2)
+        rope_mul(a)
+        evac_s(z, 0)
+        rope_add(a)
+        quant_q(a, "l")
+        new_q(z)
+        lg[z] = qt[z][:, 0:W4]
+        rope_mm(z)
+        kv_mm(a - 1, 0)
+        kv_mm(a - 1, 1)
+        evac_v(a, 3)
+        inter(a, 0, "g")
+        inter(a, 1, "g")
+        inter(a, 2, "g")
+        rope_evac(z)
+        evac_s(z, 2)
+        lat_tile(z, 2)
+        kv_evac(a - 1, 0)
+        store_n1(a - 1)
+        rope_trans(z)
+        evac_v(z, 2)
+        kv_mm(a - 1, 2)
+        kv_evac(a - 1, 1)
+        rope_mul(z)
+        lat_tile(z, 3)
+        kv_evac(a - 1, 2)
+        store_v(a - 1)
+        store_k0(a - 1)
+        store_r1(a - 1)
+        inter(z, 0, "v")
+        quant_q(z)
+        inter(z, 1, "v")
+        evac_v(z, 3)
+        kv_mm(a, 0)
+        kv_mm(a, 1)
+        rope_add(z)
+        dup_v(z)
+        kv_evac(a, 0)
+        quant_last(z, 0)
+        kv_mm(a, 2)
+        store_n1(a)
+        kv_evac(a, 1)
+        store_k0(a)
+        store_r1(a)
+        kv_half(z, 0)
+        kv_evac(a, 2)
+        store_v(a)
+        quant_last(z, 1)
+        nope_half(z, 0, "v")
+        kv_evac(z, 1)
+        store_half(z, 0)
+        storev_half(z, 0)
+        kv_half(z, 1)
+        nope_half(z, 1, "v")
+        kv_evac(z, 2)
+        store_half(z, 1)
+        storev_half(z, 1)

@@ -22,7 +22,7 @@ TPP = S // P
 TB = 4
 NB = TPP // TB
 CHUNK = 8
-WV = 512
+
 
 FLOPS = 2 * S * K * (R + ROPE) + 2 * S * R * NH * (NOPE + VD)
 
@@ -185,15 +185,16 @@ def tile_gptossmlaattention_pa_t_kernel(tc, x_bytes, x_scale, cos, sin, wkva, bk
         def quant_q(i, part="xl"):
             n = TB * P
             if "x" in part or i + 1 >= NB:
-                t_qc = p2.tile([P, 2 * TB * P], U32, align_bytes=64, name="t_qc")
-                t_qs = p2.tile([P, 2 * TB * P], U8, align_bytes=64, name="t_qs")
+                t_qc = p3.tile([P, 2 * TB * P], U32, align_bytes=64, name="t_qc")
+                t_qs = p3.tile([P, 2 * TB * P], U8, align_bytes=64, name="t_qs")
                 qc[i] = t_qc, t_qs
             t_qc, t_qs = qc[i]
             xc[i + 1], xs[i + 1] = t_qc[:, 0:n], t_qs[:, 0:n]
             lc[i - 1], ls[i - 1] = t_qc[:, n:], t_qs[:, n:]
             lo = 0 if ok(i + 1) and "x" in part else n
             hi = 2 * n if ok(i - 1) and "l" in part else n
-            quant(t_qc[:, lo:hi], t_qs[:, lo:hi], qt[i][:, 4 * lo : 4 * hi])
+            if hi > lo and (part != "l" or ok(i - 1)):
+                quant(t_qc[:, lo:hi], t_qs[:, lo:hi], qt[i][:, 4 * lo : 4 * hi])
 
         def quant_last(i, h):
             n = TB * P // 2
@@ -253,17 +254,26 @@ def tile_gptossmlaattention_pa_t_kernel(tc, x_bytes, x_scale, cos, sin, wkva, bk
             g, o = divmod(b * TB, CHUNK)
             return tiles[g][:].rearrange("p (s c) -> p s c", c=ROPE)[:, o : o + TB, :]
 
-        def rope_mul(b):
+        def rope_m1(b):
             if not ok(b):
                 return
             t_m1 = p2.tile([P, TB, ROPE], F32, name="t_m1")
+            m1[b] = t_m1
+            nc.vector.tensor_tensor(out=t_m1[:], in0=rps[b][:].rearrange("p (j c) -> p j c", c=ROPE), in1=cs(b, c_sb), op=MULT)
+
+        def rope_m2(b):
+            if not ok(b):
+                return
             t_m2 = p2.tile([P, TB, ROPE], F32, name="t_m2")
-            m1[b], m2[b] = t_m1, t_m2
-            k = rps[b][:].rearrange("p (j c) -> p j c", c=ROPE)
-            c, s = cs(b, c_sb), cs(b, s_sb)
-            nc.vector.tensor_tensor(out=t_m1[:], in0=k, in1=c, op=MULT)
-            nc.vector.tensor_tensor(out=t_m2[:].rearrange("p j (h c) -> p j h c", h=2), in0=k.rearrange("p j (h c) -> p j h c", h=2)[:, :, ::-1, :],
-                                    in1=s.rearrange("p j (h c) -> p j h c", h=2), op=MULT)
+            m2[b] = t_m2
+            nc.vector.tensor_tensor(
+                out=t_m2[:].rearrange("p j (h c) -> p j h c", h=2),
+                in0=rps[b][:].rearrange("p (j h c) -> p j h c", h=2, c=HALF)[:, :, ::-1, :],
+                in1=cs(b, s_sb).rearrange("p j (h c) -> p j h c", h=2), op=MULT)
+
+        def rope_mul(b):
+            rope_m1(b)
+            rope_m2(b)
 
         def rope_add(b):
             if not ok(b):
@@ -295,6 +305,18 @@ def tile_gptossmlaattention_pa_t_kernel(tc, x_bytes, x_scale, cos, sin, wkva, bk
                 nc.gpsimd.tensor_scalar(out=dst, in0=src, scalar1=1.0, scalar2=0.0, op0=MULT, op1=ADD)
             else:
                 nc.vector.tensor_copy(out=dst, in_=src)
+
+        def inter2(b):
+            if not ok(b):
+                return
+            nc.gpsimd.tensor_scalar(out=lg[b][:, 0 : 8 * P].rearrange("p (n t) -> p n t", t=4), in0=lpl[b][:, :, 0 : 2 * P].rearrange("p t n -> p n t"),
+                                    scalar1=1.0, scalar2=0.0, op0=MULT, op1=ADD)
+
+        def inter3(b):
+            if not ok(b):
+                return
+            nc.gpsimd.tensor_scalar(out=lg[b][:, 8 * P : 12 * P].rearrange("p (n t) -> p n t", t=4), in0=lpl[b][:, :, 2 * P : 3 * P].rearrange("p t n -> p n t"),
+                                    scalar1=1.0, scalar2=0.0, op0=MULT, op1=ADD)
 
         def evac_v(b, j):
             if not ok(b):
@@ -392,10 +414,7 @@ def tile_gptossmlaattention_pa_t_kernel(tc, x_bytes, x_scale, cos, sin, wkva, bk
 
         def casts(b):
             cast(b, 0, 1024, "s")
-            cast(b, 1024, 2048 - WV, "s")
-
-        def cast_v(b):
-            cast(b, 2048 - WV, 2048, "v")
+            cast(b, 1024, 2048, "s")
 
         new_q(-1)
         cast(0, 0, 1024, "v")
@@ -409,10 +428,11 @@ def tile_gptossmlaattention_pa_t_kernel(tc, x_bytes, x_scale, cos, sin, wkva, bk
         prep_wa(3, "s")
         mulx(0, 1)
         prep_wa(0, "v")
-        casts(1)
+        cast(1, 0, 1024, "s")
+        cast(1, 1024, 1536, "s")
         quant_q(-1)
         quant_wa()
-        cast_v(1)
+        cast(1, 1536, 2048, "v")
         quant_wr()
         trans(1, 0)
         trans(1, 1)
@@ -423,47 +443,44 @@ def tile_gptossmlaattention_pa_t_kernel(tc, x_bytes, x_scale, cos, sin, wkva, bk
         lat_pair(0, 2)
         rope_evac(0)
         evac_s(0, 0)
-        lat_tile(0, 2)
         rope_trans(0)
         evac_s(0, 2)
         mulx(1, 1)
         prep_wb()
-        lat_tile(0, 3)
-        casts(2)
-        evac_s1(0, 2)
-        cast_v(2)
+        cast(2, 0, 1024, "s")
+        cast(2, 1024, 2048, "s")
         trans(2, 0)
         trans(2, 1)
         casts(3)
         for i in range(NB - 2):
             new_kk(i)
-            cast_v(i + 3)
-            quant_q(i)
+            quant_q(i, "x")
+            quant_q(i, "l")
+            lat_tile(i, 2)
             lat_pair(i + 1, 0)
-            kv_mm(i - 1, 1)
             kv_mm(i - 1, 0)
             lat_pair(i + 1, 2)
+            kv_mm(i - 1, 1)
             new_q(i + 1)
             evac_s(i + 1, 0)
-            inter(i, 0, "g")
-            inter(i, 1, "g")
-            inter(i, 2, "g")
             kv_evac(i - 1, 0)
-            rope_mul(i)
-            evac_s(i + 1, 2)
+            inter2(i)
+            rope_m1(i)
+            rope_m2(i)
             mulx(i + 2, 0)
+            evac_s(i + 1, 2)
             rope_add(i)
             rope_mm(i + 1)
             store_n1(i - 1)
-            lat_tile(i + 1, 2)
-            kv_mm(i - 1, 2)
+            lat_tile(i, 3)
             kv_evac(i - 1, 1)
             rope_evac(i + 1)
-            evac_s1(i + 1, 2)
+            kv_mm(i - 1, 2)
+            evac_v(i, 2)
+            mulx(i + 2, 1)
             evac_v(i, 3)
             kv_evac(i - 1, 2)
             store_v(i - 1)
-            mulx(i + 2, 1)
             if i == 0:
                 quant_wb()
             trans(i + 3, 0)
@@ -471,67 +488,67 @@ def tile_gptossmlaattention_pa_t_kernel(tc, x_bytes, x_scale, cos, sin, wkva, bk
             trans(i + 3, 1)
             casts(i + 4)
             store_k0(i - 1)
-            lat_tile(i + 1, 3)
             store_r1(i - 1)
         a, z = NB - 2, NB - 1
-        new_kk(a)
-        new_kk(z)
         quant_q(a, "x")
-        lat_pair(z, 0)
-        lat_pair(z, 2)
-        rope_mul(a)
-        evac_s(z, 0)
-        rope_add(a)
         quant_q(a, "l")
+        rope_mul(a)
         new_q(z)
-        lg[z] = qt[z][:, 0:W4]
-        rope_mm(z)
-        kv_mm(a - 1, 0)
-        kv_mm(a - 1, 1)
-        evac_v(a, 3)
-        inter(a, 0, "g")
-        inter(a, 1, "g")
-        inter(a, 2, "g")
-        rope_evac(z)
-        evac_s(z, 2)
-        lat_tile(z, 2)
-        kv_evac(a - 1, 0)
-        store_n1(a - 1)
-        rope_trans(z)
-        evac_v(z, 2)
-        kv_mm(a - 1, 2)
-        kv_evac(a - 1, 1)
-        rope_mul(z)
-        lat_tile(z, 3)
-        kv_evac(a - 1, 2)
-        store_v(a - 1)
-        store_k0(a - 1)
+        lat_pair(z, 0)
         store_r1(a - 1)
-        inter(z, 0, "v")
-        quant_q(z)
+        new_kk(z)
+        inter2(a)
+        lat_pair(z, 2)
+        evac_s(z, 0)
+        lg[z] = qt[z][:, 0:W4]
+        lat_tile(a, 3)
+        evac_s(z, 2)
+        evac_v(a, 3)
+        kv_mm(a - 1, 0)
+        kv_evac(a - 1, 0)
+        new_kk(a)
+        rope_mm(z)
+        lat_tile(a, 2)
+        rope_add(a)
+        evac_v(a, 2)
+        rope_evac(z)
+        kv_mm(a - 1, 2)
+        kv_mm(a - 1, 1)
+        rope_trans(z)
         inter(z, 1, "v")
-        evac_v(z, 3)
-        kv_mm(a, 0)
+        quant_q(z)
         kv_mm(a, 1)
+        rope_mul(z)
+        kv_evac(a - 1, 2)
+        lat_tile(z, 3)
+        kv_mm(a, 0)
+        kv_evac(a - 1, 1)
+        inter(z, 0, "v")
+        store_n1(a - 1)
+        kv_mm(a, 2)
+        quant_last(z, 0)
+        store_k0(a - 1)
+        store_v(a - 1)
+        lat_tile(z, 2)
+        evac_v(z, 3)
+        store_r1(a)
+        evac_v(z, 2)
+        kv_evac(a, 1)
+        quant_last(z, 1)
+        kv_evac(a, 0)
         rope_add(z)
         dup_v(z)
-        kv_evac(a, 0)
-        quant_last(z, 0)
-        kv_mm(a, 2)
-        store_n1(a)
-        kv_evac(a, 1)
-        store_k0(a)
-        store_r1(a)
-        kv_half(z, 0)
         kv_evac(a, 2)
+        store_k0(a)
+        kv_half(z, 0)
         store_v(a)
-        quant_last(z, 1)
-        nope_half(z, 0, "v")
-        kv_evac(z, 1)
-        store_half(z, 0)
-        storev_half(z, 0)
         kv_half(z, 1)
-        nope_half(z, 1, "v")
-        kv_evac(z, 2)
+        store_n1(a)
+        nope_half(z, 0, "s")
+        kv_evac(z, 1)
+        nope_half(z, 1, "s")
+        storev_half(z, 0)
+        store_half(z, 0)
         store_half(z, 1)
+        kv_evac(z, 2)
         storev_half(z, 1)

from contextlib import ExitStack

import concourse.mybir as mybir
from concourse.masks import make_identity

F32 = mybir.dt.float32
BF16 = mybir.dt.bfloat16
U32 = mybir.dt.uint32
U8 = mybir.dt.uint8
FP8 = mybir.dt.float8_e4m3fn
FP8X4 = mybir.dt.float8_e4m3fn_x4
MULT = mybir.AluOpType.mult
ADD = mybir.AluOpType.add
SUB = mybir.AluOpType.subtract
IDENT = mybir.ActivationFunctionType.Identity

P = 128
S, K, R = 8192, 512, 512
ROPE, NOPE, VD, NH = 128, 64, 128, 2
HALF = ROPE // 2
TPP = S // P
TB = 4
NB = TPP // TB
CHUNK = 8


FLOPS = 2 * S * K * (R + ROPE) + 2 * S * R * NH * (NOPE + VD)


def tile_gptossmlaattention_pa_t_kernel(tc, x_bytes, x_scale, cos, sin, wkva, bkva, wkvb, kk_out, v_out):
    nc = tc.nc
    with ExitStack() as ctx:
        ctx.enter_context(tc.manual_schedule())
        keep = ctx.enter_context(tc.tile_pool(name="keep", bufs=1))
        p2 = ctx.enter_context(tc.tile_pool(name="p2", bufs=2))
        p3 = ctx.enter_context(tc.tile_pool(name="p3", bufs=3))
        plg = ctx.enter_context(tc.tile_pool(name="plg", bufs=1))
        outp = ctx.enter_context(tc.tile_pool(name="outp", bufs=4))
        ps_x = ctx.enter_context(tc.psum_pool(name="ps_x", bufs=2))
        ps_l = ctx.enter_context(tc.psum_pool(name="ps_l", bufs=3))
        ps_r = ctx.enter_context(tc.psum_pool(name="ps_r", bufs=1))
        ps_kv = ctx.enter_context(tc.psum_pool(name="ps_kv", bufs=2))

        x_rows = x_bytes.rearrange("o (p s) k -> p (o s k)", p=P)
        cos_rows = cos.rearrange("o (p s) c -> p (o s c)", p=P)
        sin_rows = sin.rearrange("o (p s) c -> p (o s c)", p=P)
        kk_rows = kk_out.rearrange("o h (p s) c -> p (o h) (s c)", p=P)
        kk1_rows = kk_out[:, 1].rearrange("o (p s) c -> p (o s) c", p=P)
        v_rows = v_out.rearrange("o h (p s) c -> p (o h) (s c)", p=P)

        x_sb, c_sb, s_sb = [], [], []
        for g in range(TPP // CHUNK):
            xt = keep.tile([P, CHUNK * K], U8, name="x%d" % g)
            ct = keep.tile([P, CHUNK * ROPE], BF16, name="c%d" % g)
            st = keep.tile([P, CHUNK * ROPE], BF16, name="s%d" % g)
            x_sb.append(xt)
            c_sb.append(ct)
            s_sb.append(st)

        def load_x(g, lo, hi):
            nc.sync.dma_start(out=x_sb[g][:, lo * K : hi * K], in_=x_rows[:, (g * CHUNK + lo) * K : (g * CHUNK + hi) * K])

        def load_cs(g):
            cols = slice(g * CHUNK * ROPE, (g + 1) * CHUNK * ROPE)
            nc.sync.dma_start(out=c_sb[g][:], in_=cos_rows[:, cols])
            nc.sync.dma_start(out=s_sb[g][:], in_=sin_rows[:, cols])

        wa_raw = keep.tile([P, 4, R + ROPE], BF16, name="wa_raw")
        wb_raw = keep.tile([P, 4, NH * (NOPE + VD)], BF16, name="wb_raw")
        scale = keep.tile([P, 4], F32, name="scale")
        bias_l = keep.tile([P, 4], BF16, name="bias_l")
        bias_r = keep.tile([P, 1], BF16, name="bias_r")
        load_x(0, 0, 2)
        nc.sync.dma_start(out=scale[:], in_=x_scale.rearrange("a b (p t) -> p (a b t)", t=4))
        load_x(0, 2, 4)
        nc.sync.dma_start(out=wa_raw[:], in_=wkva.rearrange("(p j) w -> p j w", j=4))
        load_x(0, 4, 8)
        nc.sync.dma_start(out=bias_l[:], in_=bkva[0:R].rearrange("(p t) -> p t", t=4))
        nc.sync.dma_start(out=bias_r[:], in_=bkva[R : R + ROPE].rearrange("(p o) -> p o", o=1))
        load_x(1, 0, CHUNK)
        load_cs(0)
        nc.sync.dma_start(out=wb_raw[:], in_=wkvb.rearrange("(p j) w -> p j w", j=4))
        load_cs(1)
        for g in range(2, TPP // CHUNK):
            load_x(g, 0, CHUNK)
            load_cs(g)
        warm = keep.tile([P, 1], F32, name="warm")
        nc.vector.memset(warm[:], 0.0)
        nc.scalar.activation(out=warm[:], in_=warm[:], func=IDENT)
        ident = keep.tile([P, P], F32, name="ident")
        make_identity(nc, ident[:])

        wa_g = keep.tile([P, R * 4], BF16, align_bytes=64, name="wa_g")
        wr_g = keep.tile([P, ROPE * 4], BF16, align_bytes=64, name="wr_g")
        wn_g = keep.tile([P, NH * NOPE * 4], BF16, align_bytes=64, name="wn_g")
        wv_g = keep.tile([P, NH * VD * 4], BF16, align_bytes=64, name="wv_g")
        wa_c = keep.tile([P, R], U32, align_bytes=64, name="wa_c")
        wa_s = keep.tile([P, R], U8, align_bytes=64, name="wa_s")
        wr_c = keep.tile([P, ROPE], U32, align_bytes=64, name="wr_c")
        wr_s = keep.tile([P, ROPE], U8, align_bytes=64, name="wr_s")
        wn_c = keep.tile([P, NH * NOPE], U32, align_bytes=64, name="wn_c")
        wn_s = keep.tile([P, NH * NOPE], U8, align_bytes=64, name="wn_s")
        wv_c = keep.tile([P, NH * VD], U32, align_bytes=64, name="wv_c")
        wv_s = keep.tile([P, NH * VD], U8, align_bytes=64, name="wv_s")

        def quant(codes, scales, src):
            nc.vector.quantize_mx(out=codes.bitcast(FP8X4), scales=scales, in_=src)

        def prep_wa(t, eng):
            src = wa_raw[:, :, 0:R].rearrange("p j (m t) -> p t m j", t=4)
            dst = wa_g[:].rearrange("p (t m j) -> p t m j", t=4, j=4)
            copy = nc.scalar.copy if eng == "s" else nc.vector.tensor_copy
            copy(out=dst[:, t], in_=src[:, t])

        def prep_wr():
            nc.gpsimd.tensor_scalar(out=wr_g[:].rearrange("p (c j) -> p c j", j=4), in0=wa_raw[:, :, R:].rearrange("p j c -> p c j"),
                                    scalar1=1.0, scalar2=0.0, op0=MULT, op1=ADD)

        def quant_wa():
            quant(wa_c[:], wa_s[:], wa_g[:])

        def quant_wr():
            quant(wr_c[:], wr_s[:], wr_g[:])

        def prep_wb():
            src = wb_raw[:].rearrange("p j (h w) -> p h w j", h=NH)
            for h in range(NH):
                nc.gpsimd.tensor_scalar(out=wn_g[:].rearrange("p (h c j) -> p h c j", h=NH, j=4)[:, h], in0=src[:, h, 0:NOPE],
                                        scalar1=1.0, scalar2=0.0, op0=MULT, op1=ADD)
                nc.gpsimd.tensor_scalar(out=wv_g[:].rearrange("p (h c j) -> p h c j", h=NH, j=4)[:, h], in0=src[:, h, NOPE:],
                                        scalar1=1.0, scalar2=0.0, op0=MULT, op1=ADD)

        def quant_wb():
            quant(wn_c[:], wn_s[:], wn_g[:])
            quant(wv_c[:], wv_s[:], wv_g[:])

        qt, qc, xw, xps, xg, xc, xs = {}, {}, {}, {}, {}, {}, {}
        lps, lpl, lg, lc, ls = {}, {}, {}, {}, {}
        rps, kt, m1, m2, kvps, kk, vt = {}, {}, {}, {}, {}, {}, {}

        def ok(b):
            return 0 <= b < NB

        def cast(b, c0, c1, eng):
            if not ok(b):
                return
            if c0 == 0:
                t_xw = p3.tile([P, TB, K], BF16, align_bytes=64, name="t_xw")
                xw[b] = t_xw
            g, o = divmod(b * TB, CHUNK)
            src = x_sb[g][:, o * K + c0 : o * K + c1].bitcast(FP8)
            dst = xw[b][:].rearrange("p j k -> p (j k)")[:, c0:c1]
            if eng == "v":
                nc.vector.tensor_copy(out=dst, in_=src)
            else:
                nc.scalar.copy(out=dst, in_=src)

        def trans(b, h):
            if not ok(b):
                return
            t_xps = ps_x.tile([P, 2, 2 * P], F32, name="t_xps")
            xps[b, h] = t_xps
            for jj in range(2):
                words = xw[b][:, 2 * h + jj, :].bitcast(F32)
                for u in range(2):
                    nc.tensor.transpose(t_xps[:, u, jj * P : (jj + 1) * P], words[:, u : K // 2 : 2], ident[:])

        def mulx(b, h):
            if not ok(b):
                return
            nc.vector.tensor_tensor(
                out=xg[b][:, h * 1024 : (h + 1) * 1024].rearrange("p (c u e) -> p c u e", u=2, e=2),
                in0=xps[b, h][:].bitcast(BF16).rearrange("p u (c e) -> p c u e", e=2),
                in1=scale[:].unsqueeze(1).to_broadcast([P, 2 * P, 4]).rearrange("p c (u e) -> p c u e", e=2),
                op=MULT,
            )

        W4 = TB * P * 4

        def new_q(i):
            t_q = plg.tile([P, 2 * W4], BF16, align_bytes=64, name="t_q")
            qt[i] = t_q
            xg[i + 1], lg[i - 1] = t_q[:, 0:W4], t_q[:, W4:]

        def quant_q(i, part="xl"):
            n = TB * P
            if "x" in part or i + 1 >= NB:
                t_qc = p3.tile([P, 2 * TB * P], U32, align_bytes=64, name="t_qc")
                t_qs = p3.tile([P, 2 * TB * P], U8, align_bytes=64, name="t_qs")
                qc[i] = t_qc, t_qs
            t_qc, t_qs = qc[i]
            xc[i + 1], xs[i + 1] = t_qc[:, 0:n], t_qs[:, 0:n]
            lc[i - 1], ls[i - 1] = t_qc[:, n:], t_qs[:, n:]
            lo = 0 if ok(i + 1) and "x" in part else n
            hi = 2 * n if ok(i - 1) and "l" in part else n
            if hi > lo and (part != "l" or ok(i - 1)):
                quant(t_qc[:, lo:hi], t_qs[:, lo:hi], qt[i][:, 4 * lo : 4 * hi])

        def quant_last(i, h):
            n = TB * P // 2
            t_qc, t_qs = qc[i]
            lc[i], ls[i] = t_qc[:, 0 : 2 * n], t_qs[:, 0 : 2 * n]
            quant(t_qc[:, h * n : (h + 1) * n], t_qs[:, h * n : (h + 1) * n], qt[i][:, 4 * h * n : 4 * (h + 1) * n])

        def lat_pair(b, t0):
            if not ok(b):
                return
            t_lps = ps_l.tile([P, 2, 2 * P], F32, name="t_lps")
            lps[b, "s", t0] = t_lps
            for t in (t0, t0 + 1):
                w = slice(t * P, (t + 1) * P)
                nc.tensor.matmul_mx(
                    out=t_lps[:, t - t0, :], lhsT=wa_c[:, w].bitcast(FP8X4), lhsT_scale=wa_s[:, w],
                    rhs=xc[b][:, 0 : 2 * P].bitcast(FP8X4), rhs_scale=xs[b][:, 0 : 2 * P], start=True, stop=True)

        def lat_tile(b, j):
            if not ok(b):
                return
            t_lps = ps_l.tile([P, 4, P], F32, name="t_lps")
            lps[b, "v", j] = t_lps
            n = slice(j * P, (j + 1) * P)
            for t in range(4):
                w = slice(t * P, (t + 1) * P)
                nc.tensor.matmul_mx(
                    out=t_lps[:, t, :], lhsT=wa_c[:, w].bitcast(FP8X4), lhsT_scale=wa_s[:, w],
                    rhs=xc[b][:, n].bitcast(FP8X4), rhs_scale=xs[b][:, n], start=True, stop=True)

        def rope_mm(b):
            if not ok(b):
                return
            t_rps = ps_r.tile([P, TB * P], F32, name="t_rps")
            rps[b] = t_rps
            nc.tensor.matmul_mx(
                out=t_rps[:], lhsT=wr_c[:].bitcast(FP8X4), lhsT_scale=wr_s[:],
                rhs=xc[b].bitcast(FP8X4), rhs_scale=xs[b], start=True, stop=True)

        def rope_evac(b):
            if not ok(b):
                return
            t_kt = p2.tile([P, TB * P], F32, name="t_kt")
            kt[b] = t_kt
            nc.scalar.activation(out=t_kt[:], in_=rps[b][:], func=IDENT, bias=bias_r[:])

        def rope_trans(b):
            if not ok(b):
                return
            t_rps = ps_r.tile([P, TB * P], F32, name="t_rps")
            rps[b] = t_rps
            for j in range(TB):
                n = slice(j * P, (j + 1) * P)
                nc.tensor.transpose(t_rps[:, n], kt[b][:, n], ident[:])

        def cs(b, tiles):
            g, o = divmod(b * TB, CHUNK)
            return tiles[g][:].rearrange("p (s c) -> p s c", c=ROPE)[:, o : o + TB, :]

        def rope_m1(b):
            if not ok(b):
                return
            t_m1 = p2.tile([P, TB, ROPE], F32, name="t_m1")
            m1[b] = t_m1
            nc.vector.tensor_tensor(out=t_m1[:], in0=rps[b][:].rearrange("p (j c) -> p j c", c=ROPE), in1=cs(b, c_sb), op=MULT)

        def rope_m2(b):
            if not ok(b):
                return
            t_m2 = p2.tile([P, TB, ROPE], F32, name="t_m2")
            m2[b] = t_m2
            nc.vector.tensor_tensor(
                out=t_m2[:].rearrange("p j (h c) -> p j h c", h=2),
                in0=rps[b][:].rearrange("p (j h c) -> p j h c", h=2, c=HALF)[:, :, ::-1, :],
                in1=cs(b, s_sb).rearrange("p j (h c) -> p j h c", h=2), op=MULT)

        def rope_mul(b):
            rope_m1(b)
            rope_m2(b)

        def rope_add(b):
            if not ok(b):
                return
            nc.gpsimd.tensor_tensor(out=kk[b][:, 0, :, NOPE : NOPE + HALF], in0=m1[b][:, :, 0:HALF], in1=m2[b][:, :, 0:HALF], op=SUB)
            nc.gpsimd.tensor_tensor(out=kk[b][:, 0, :, NOPE + HALF :], in0=m1[b][:, :, HALF:], in1=m2[b][:, :, HALF:], op=ADD)

        def evac_s(b, t0):
            if not ok(b):
                return
            if t0 == 0:
                t_lpl = p2.tile([P, 4, 3 * P], BF16, align_bytes=64, name="t_lpl")
                lpl[b] = t_lpl
            for t in (t0, t0 + 1):
                nc.scalar.activation(out=lpl[b][:, t, 0 : 2 * P], in_=lps[b, "s", t0][:, t - t0, :], func=IDENT, bias=bias_l[:, t : t + 1])

        def evac_s1(b, j):
            if not ok(b):
                return
            for t in range(4):
                nc.scalar.activation(out=lpl[b][:, t, j * P : (j + 1) * P], in_=lps[b, "v", j][:, t, :], func=IDENT, bias=bias_l[:, t : t + 1])

        def inter(b, j, eng):
            if not ok(b):
                return
            dst = lg[b][:, j * 512 : (j + 1) * 512].rearrange("p (n t) -> p n t", t=4)
            src = lpl[b][:, :, j * P : (j + 1) * P].rearrange("p t n -> p n t")
            if eng == "g":
                nc.gpsimd.tensor_scalar(out=dst, in0=src, scalar1=1.0, scalar2=0.0, op0=MULT, op1=ADD)
            else:
                nc.vector.tensor_copy(out=dst, in_=src)

        def inter2(b):
            if not ok(b):
                return
            nc.gpsimd.tensor_scalar(out=lg[b][:, 0 : 8 * P].rearrange("p (n t) -> p n t", t=4), in0=lpl[b][:, :, 0 : 2 * P].rearrange("p t n -> p n t"),
                                    scalar1=1.0, scalar2=0.0, op0=MULT, op1=ADD)

        def inter3(b):
            if not ok(b):
                return
            nc.gpsimd.tensor_scalar(out=lg[b][:, 8 * P : 12 * P].rearrange("p (n t) -> p n t", t=4), in0=lpl[b][:, :, 2 * P : 3 * P].rearrange("p t n -> p n t"),
                                    scalar1=1.0, scalar2=0.0, op0=MULT, op1=ADD)

        def evac_v(b, j):
            if not ok(b):
                return
            nc.vector.tensor_tensor(
                out=lg[b][:, j * 512 : (j + 1) * 512].rearrange("p (n t) -> p n t", t=4),
                in0=lps[b, "v", j][:].rearrange("p t n -> p n t"),
                in1=bias_l[:].unsqueeze(1).to_broadcast([P, P, 4]), op=ADD)

        def kv_mm(b, part):
            if not ok(b):
                return
            t_kv = ps_kv.tile([P, 512], F32, name="t_kv")
            kvps[b, part] = t_kv
            tiles = range(TB) if part == 0 else (2 * part - 2, 2 * part - 1)
            wc, ws, width = (wn_c, wn_s, 128) if part == 0 else (wv_c, wv_s, 256)
            for i, j in enumerate(tiles):
                n = slice(j * P, (j + 1) * P)
                nc.tensor.matmul_mx(
                    out=t_kv[:, i * width : (i + 1) * width], lhsT=lc[b][:, n].bitcast(FP8X4), lhsT_scale=ls[b][:, n],
                    rhs=wc[:].bitcast(FP8X4), rhs_scale=ws[:], start=True, stop=True)

        def kv_half(b, h):
            t_kn = ps_kv.tile([P, 512], F32, name="t_kv")
            t_kv = ps_kv.tile([P, 512], F32, name="t_kv")
            kvps[b, "n", h], kvps[b, h + 1] = t_kn, t_kv
            for dst, wc, ws, width in ((t_kn, wn_c, wn_s, 128), (t_kv, wv_c, wv_s, 256)):
                for i in range(2):
                    n = slice((2 * h + i) * P, (2 * h + i + 1) * P)
                    nc.tensor.matmul_mx(
                        out=dst[:, i * width : (i + 1) * width], lhsT=lc[b][:, n].bitcast(FP8X4), lhsT_scale=ls[b][:, n],
                        rhs=wc[:].bitcast(FP8X4), rhs_scale=ws[:], start=True, stop=True)

        def nope_half(b, h, eng):
            copy = nc.scalar.copy if eng == "s" else nc.vector.tensor_copy
            copy(out=kk[b][:, :, 2 * h : 2 * h + 2, 0:NOPE].rearrange("p h j c -> p j h c"),
                 in_=kvps[b, "n", h][:, 0 : 2 * P].rearrange("p (j h c) -> p j h c", j=2, h=NH))

        def store_half(b, h):
            w = 2 * (NOPE + ROPE)
            o = b * 2 * w + h * w
            nc.sync.dma_start(out=kk_rows[:, :, o : o + w], in_=kk[b][:, :, 2 * h : 2 * h + 2, :].rearrange("p h j c -> p h (j c)"))

        def storev_half(b, h):
            w = 2 * VD
            o = b * 2 * w + h * w
            nc.sync.dma_start(out=v_rows[:, :, o : o + w], in_=vt[b][:, :, 2 * h : 2 * h + 2, :].rearrange("p h j c -> p h (j c)"))

        def new_kk(b):
            if not ok(b):
                return
            t_kk = outp.tile([P, NH, TB, NOPE + ROPE], F32, name="t_kk")
            t_v = outp.tile([P, NH, TB, VD], F32, name="t_v")
            kk[b], vt[b] = t_kk, t_v

        def kv_evac(b, part, eng="s"):
            if not ok(b):
                return
            copy = nc.scalar.copy if eng == "s" else nc.vector.tensor_copy
            if part == 0:
                copy(out=kk[b][:, :, :, 0:NOPE].rearrange("p h j c -> p j h c"),
                     in_=kvps[b, 0][:].rearrange("p (j h c) -> p j h c", j=TB, h=NH))
            else:
                copy(out=vt[b][:, :, 2 * part - 2 : 2 * part, :].rearrange("p h j c -> p j h c"),
                     in_=kvps[b, part][:].rearrange("p (j h c) -> p j h c", j=2, h=NH))

        def dup_v(b):
            nc.gpsimd.tensor_scalar(out=kk[b][:, 1, :, NOPE:], in0=kk[b][:, 0, :, NOPE:], scalar1=1.0, scalar2=0.0, op0=MULT, op1=ADD)

        def store_k01(b):
            w = TB * (NOPE + ROPE)
            nc.sync.dma_start(out=kk_rows[:, :, b * w : (b + 1) * w], in_=kk[b][:].rearrange("p h j c -> p h (j c)"))

        def store_v(b):
            if not ok(b):
                return
            w = TB * VD
            nc.sync.dma_start(out=v_rows[:, :, b * w : (b + 1) * w], in_=vt[b][:].rearrange("p h j c -> p h (j c)"))

        def store_k0(b):
            if not ok(b):
                return
            w = TB * (NOPE + ROPE)
            nc.sync.dma_start(out=kk_rows[:, 0, b * w : (b + 1) * w], in_=kk[b][:, 0].rearrange("p j c -> p (j c)"))

        def store_r1(b):
            if not ok(b):
                return
            nc.sync.dma_start(out=kk1_rows[:, b * TB : (b + 1) * TB, NOPE:], in_=kk[b][:, 0, :, NOPE:])

        def store_n1(b):
            if not ok(b):
                return
            nc.sync.dma_start(out=kk1_rows[:, b * TB : (b + 1) * TB, 0:NOPE], in_=kk[b][:, 1, :, 0:NOPE])

        def casts(b):
            cast(b, 0, 1024, "s")
            cast(b, 1024, 2048, "s")

        new_q(-1)
        cast(0, 0, 1024, "v")
        cast(0, 1024, 2048, "s")
        trans(0, 0)
        trans(0, 1)
        mulx(0, 0)
        prep_wr()
        prep_wa(1, "s")
        prep_wa(2, "s")
        prep_wa(3, "s")
        mulx(0, 1)
        prep_wa(0, "v")
        cast(1, 0, 1024, "s")
        cast(1, 1024, 1536, "s")
        quant_q(-1)
        quant_wa()
        cast(1, 1536, 2048, "v")
        quant_wr()
        trans(1, 0)
        trans(1, 1)
        new_q(0)
        mulx(1, 0)
        rope_mm(0)
        lat_pair(0, 0)
        lat_pair(0, 2)
        rope_evac(0)
        evac_s(0, 0)
        rope_trans(0)
        evac_s(0, 2)
        mulx(1, 1)
        prep_wb()
        cast(2, 0, 1024, "s")
        cast(2, 1024, 2048, "s")
        trans(2, 0)
        trans(2, 1)
        casts(3)
        for i in range(NB - 2):
            new_kk(i)
            quant_q(i, "x")
            quant_q(i, "l")
            lat_tile(i, 2)
            lat_pair(i + 1, 0)
            kv_mm(i - 1, 0)
            lat_pair(i + 1, 2)
            kv_mm(i - 1, 1)
            new_q(i + 1)
            evac_s(i + 1, 0)
            kv_evac(i - 1, 0)
            inter2(i)
            rope_m1(i)
            rope_m2(i)
            mulx(i + 2, 0)
            evac_s(i + 1, 2)
            rope_add(i)
            rope_mm(i + 1)
            store_n1(i - 1)
            lat_tile(i, 3)
            kv_evac(i - 1, 1)
            rope_evac(i + 1)
            kv_mm(i - 1, 2)
            evac_v(i, 2)
            mulx(i + 2, 1)
            evac_v(i, 3)
            kv_evac(i - 1, 2)
            store_v(i - 1)
            if i == 0:
                quant_wb()
            trans(i + 3, 0)
            rope_trans(i + 1)
            trans(i + 3, 1)
            casts(i + 4)
            store_k0(i - 1)
            store_r1(i - 1)
        a, z = NB - 2, NB - 1
        quant_q(a, "x")
        quant_q(a, "l")
        rope_mul(a)
        new_q(z)
        lat_pair(z, 0)
        store_r1(a - 1)
        new_kk(z)
        inter2(a)
        lat_pair(z, 2)
        evac_s(z, 0)
        lg[z] = qt[z][:, 0:W4]
        lat_tile(a, 3)
        evac_s(z, 2)
        evac_v(a, 3)
        kv_mm(a - 1, 0)
        kv_evac(a - 1, 0)
        new_kk(a)
        rope_mm(z)
        lat_tile(a, 2)
        rope_add(a)
        evac_v(a, 2)
        rope_evac(z)
        kv_mm(a - 1, 2)
        kv_mm(a - 1, 1)
        rope_trans(z)
        inter(z, 1, "v")
        quant_q(z)
        kv_mm(a, 1)
        rope_mul(z)
        kv_evac(a - 1, 2)
        lat_tile(z, 3)
        kv_mm(a, 0)
        kv_evac(a - 1, 1)
        inter(z, 0, "v")
        store_n1(a - 1)
        kv_mm(a, 2)
        quant_last(z, 0)
        store_k0(a - 1)
        store_v(a - 1)
        lat_tile(z, 2)
        evac_v(z, 3)
        store_r1(a)
        evac_v(z, 2)
        kv_evac(a, 1)
        quant_last(z, 1)
        kv_evac(a, 0)
        rope_add(z)
        dup_v(z)
        kv_evac(a, 2)
        store_k0(a)
        kv_half(z, 0)
        store_v(a)
        kv_half(z, 1)
        store_n1(a)
        nope_half(z, 0, "s")
        kv_evac(z, 1)
        nope_half(z, 1, "s")
        storev_half(z, 0)
        store_half(z, 0)
        store_half(z, 1)
        kv_evac(z, 2)
        storev_half(z, 1)
